import numpy as np
import ml_dtypes


def mxq(x, axis, fmt="e4m3"):
    dtype, down = {"e4m3": (ml_dtypes.float8_e4m3fn, 7), "e5m2": (ml_dtypes.float8_e5m2, 14)}[fmt]
    v = np.moveaxis(np.asarray(x, np.float32).astype(ml_dtypes.bfloat16).astype(np.float64), axis, -1)
    blocks = v.reshape(v.shape[:-1] + (-1, 32))
    amax = np.abs(blocks).max(-1, keepdims=True)
    byte = np.maximum(np.where(amax > 0, np.frexp(amax)[1] - 1 + 127, 0) - down, 1)
    scale = np.exp2(byte - 127.0)
    codes = (blocks / scale).astype(np.float32).astype(dtype).astype(np.float64)
    return np.moveaxis((codes * scale).reshape(v.shape), -1, axis)


WIDE = False


def mx_kscale(k):
    if not WIDE:
        return np.ones(k)
    levels = np.array([10, -10, 5, -5, 0])
    a = np.random.permutation(np.resize(levels, k // 512 * 4)).reshape(k // 512, 4)
    idx = np.arange(k)
    return np.exp2(a[idx // 512, idx % 128 // 32])


BF16 = ml_dtypes.bfloat16


def bf(x):
    return np.asarray(x, np.float32).astype(BF16)


def f64(x):
    return np.asarray(x).astype(np.float64)


B, SEQ, C, P, H, W = 4, 16, 128, 512, 8, 8
L = SEQ * H * W


def setup_inputs():
    s = mx_kscale(P)
    return {"att_logits": bf(np.random.standard_normal((B, L, L)) * 2.0),
            "g": bf(np.random.standard_normal((B, P, L)) * s[None, :, None]),
            "w1_w": bf(np.random.standard_normal((C, P)) / np.sqrt(P) / s[None, :]),
            "w1_b": bf(np.random.standard_normal(C) * 0.1),
            "w2_w": bf(np.random.standard_normal((C, P)) * 2.0 / np.sqrt(P) / s[None, :]),
            "w2_b": bf(np.random.standard_normal(C) * 0.1)}


def reference(att_logits, g, w1_w, w1_b, w2_w, w2_b):
    a = f64(att_logits)
    gg = f64(g)
    e = np.exp(a - a.max(-1, keepdims=True))
    y = (mxq(e, 2, "e4m3") @ mxq(gg, 2, "e4m3").transpose(0, 2, 1)) / e.sum(-1, keepdims=True)
    x2 = (mxq(y, 2, "e4m3") @ mxq(f64(w2_w), 1, "e4m3").T) + f64(w2_b)
    x1 = (mxq(gg, 1, "e4m3").transpose(0, 2, 1) @ mxq(f64(w1_w), 1, "e4m3").T) + f64(w1_b)
    return (x1 + x2).transpose(0, 2, 1)

@@ -1,0 +1,222 @@
+from contextlib import ExitStack
+
+import concourse.mybir as mybir
+from concourse.masks import make_identity
+
+F32 = mybir.dt.float32
+BF16 = mybir.dt.bfloat16
+U32 = mybir.dt.uint32
+U8 = mybir.dt.uint8
+FP8X4 = mybir.dt.float8_e4m3fn_x4
+ALU = mybir.AluOpType
+ACT = mybir.ActivationFunctionType
+AXIS = mybir.AxisListType
+
+P = 128
+PACK = 4
+K_PASS = P * PACK
+CLIPS, L, FEAT, CH = 4, 1024, 512, 128
+L_TILES = L // P
+M_PASSES = L // K_PASS
+F_TILES = FEAT // P
+ROUND = 4
+ROUNDS = L_TILES // ROUND
+FOLD_STOP = 64
+MAX_AHEAD = 2
+
+FLOPS = 2 * CLIPS * (L * L * FEAT + 2 * L * FEAT * CH)
+
+
+def tile_stnonlocalgnlstage_pb_t_kernel(tc, att_logits, g, w1_w, w1_b, w2_w, w2_b, out):
+    nc = tc.nc
+    with ExitStack() as stack:
+        const = stack.enter_context(tc.tile_pool(name="const", bufs=1))
+        inputs = stack.enter_context(tc.tile_pool(name="inputs", bufs=1))
+        work = stack.enter_context(tc.tile_pool(name="work", bufs=2))
+        psum = stack.enter_context(tc.psum_pool(name="psum", bufs=1))
+
+        a_sb = [inputs.tile([P, L_TILES, L], BF16, name="a%d" % b) for b in range(CLIPS)]
+        g_sb = [inputs.tile([P, PACK, L], BF16, name="g%d" % b) for b in range(CLIPS)]
+        w_sb = const.tile([P, 2, FEAT], BF16)
+        bias_rows = const.tile([P, P], BF16)
+
+        def load_logits(b, h):
+            tiles = slice(h * ROUND, (h + 1) * ROUND)
+            rows = att_logits[b].rearrange("(i p) m -> p i m", p=P)
+            nc.sync.dma_start(out=a_sb[b][:, tiles, :], in_=rows[:, tiles, :])
+
+        def load_values(b):
+            nc.sync.dma_start(out=g_sb[b][:], in_=g[b].rearrange("(q j) m -> q j m", j=PACK))
+
+        nc.gpsimd.memset(bias_rows[:], 0.0)
+        load_logits(0, 0)
+        load_values(0)
+        nc.sync.dma_start(out=w_sb[:, 0, :], in_=w1_w)
+        nc.sync.dma_start(out=w_sb[:, 1, :], in_=w2_w)
+        nc.sync.dma_start(out=bias_rows[0:1, :], in_=w1_b.rearrange("(o c) -> o c", o=1))
+        nc.sync.dma_start(out=bias_rows[1:2, :], in_=w2_b.rearrange("(o c) -> o c", o=1))
+        load_logits(0, 1)
+        for b in range(1, CLIPS):
+            load_values(b)
+            for h in range(ROUNDS):
+                load_logits(b, h)
+
+        ident = const.tile([P, P], F32)
+        make_identity(nc, ident[:])
+        ident_bf = const.tile([P, P], BF16)
+        make_identity(nc, ident_bf[:])
+
+        def transpose_pairs(blocks, grouped):
+            bank = psum.tile([P, 4, P], F32, tag="bank", bufs=3)
+            for n, block in enumerate(blocks):
+                nc.tensor.transpose(bank[:, n, :], block, ident[:])
+            nc.scalar.copy(out=grouped, in_=bank[:].rearrange("q (c u) r -> q c r u", u=2))
+
+        def quantise(grouped, codes, scales):
+            nc.vector.quantize_mx(out=codes.bitcast(FP8X4), scales=scales, in_=grouped)
+
+        def row_maxima(b, h):
+            src = a_sb[b][:, h * ROUND : (h + 1) * ROUND, :]
+            width = L // 2
+            while width >= FOLD_STOP:
+                fold = work.tile([P, ROUND, width], BF16, tag="fold")
+                nc.vector.tensor_tensor(
+                    out=fold[:], in0=src[:, :, 0:width], in1=src[:, :, width : 2 * width], op=ALU.max
+                )
+                src = fold
+                width //= 2
+            neg_max = work.tile([P, ROUND], F32, tag="neg_max", bufs=MAX_AHEAD + 2)
+            nc.vector.tensor_reduce(out=neg_max[:], in_=src[:], axis=AXIS.X, op=ALU.max, negate=True)
+            return neg_max
+
+        w_grouped = const.tile([P, 2 * CH * PACK], BF16, align_bytes=64)
+        w_codes = const.tile([P, 2, CH], U32, align_bytes=64)
+        w_scales = const.tile([P, 2, CH], U8, align_bytes=64)
+        w_words = w_sb[:].rearrange("c w p -> c (w p)").bitcast(F32).rearrange("c (w q u) -> c w u q", w=2, u=2)
+        transpose_pairs(
+            [w_words[:, w, u, :] for w in range(2) for u in range(2)],
+            w_grouped[:].bitcast(F32).rearrange("q (w c u) -> q w c u", w=2, u=2),
+        )
+        quantise(
+            w_grouped[:],
+            w_codes[:].rearrange("q w c -> q (w c)"),
+            w_scales[:].rearrange("q w c -> q (w c)"),
+        )
+
+        bias_cols = psum.tile([P, P], BF16, tag="bank", bufs=3)
+        nc.tensor.transpose(bias_cols[:], bias_rows[:], ident_bf[:])
+        bias = const.tile([P, 1], F32)
+        nc.vector.tensor_reduce(out=bias[:], in_=bias_cols[:, 0:2], axis=AXIS.X, op=ALU.add)
+
+        rounds = [(b, h) for b in range(CLIPS) for h in range(ROUNDS)]
+        neg_maxima = [row_maxima(b, h) for (b, h) in rounds[:MAX_AHEAD]]
+
+        for r, (b, h) in enumerate(rounds):
+            if r + MAX_AHEAD < len(rounds):
+                neg_maxima.append(row_maxima(*rounds[r + MAX_AHEAD]))
+
+            if h == 0:
+                gT_grouped = work.tile([P, M_PASSES * FEAT * PACK], BF16, align_bytes=64, bufs=1)
+                gT_codes = work.tile([P, M_PASSES, F_TILES, P], U32, align_bytes=64)
+                gT_scales = work.tile([P, M_PASSES, F_TILES, P], U8, align_bytes=64)
+                gT_words = gT_grouped[:].bitcast(F32).rearrange("q (c j f u) -> q c j f u", c=M_PASSES, j=F_TILES, u=2)
+                for j in range(F_TILES):
+                    g_words = g_sb[b][:, j, :].bitcast(F32)
+                    transpose_pairs(
+                        [g_words[:, n * P : (n + 1) * P] for n in range(4)], gT_words[:, :, j, :, :]
+                    )
+                quantise(
+                    gT_grouped[:],
+                    gT_codes[:].rearrange("q c j f -> q (c j f)"),
+                    gT_scales[:].rearrange("q c j f -> q (c j f)"),
+                )
+
+                gp_grouped = work.tile([P, L, PACK], BF16, align_bytes=64, bufs=1)
+                gp_codes = work.tile([P, L], U32, align_bytes=64)
+                gp_scales = work.tile([P, L], U8, align_bytes=64)
+                nc.vector.tensor_copy(
+                    out=gp_grouped[:].rearrange("q (n i) j -> q n j i", i=4),
+                    in_=g_sb[b][:].rearrange("q j (n i) -> q n j i", i=4),
+                )
+                quantise(gp_grouped[:].rearrange("q l j -> q (l j)"), gp_codes[:], gp_scales[:])
+
+            e_sum = work.tile([P, ROUND], F32)
+            eT_grouped = work.tile([P, ROUND, M_PASSES * P * PACK], BF16, align_bytes=64)
+            eT_codes = work.tile([P, ROUND, M_PASSES, P], U32, align_bytes=64)
+            eT_scales = work.tile([P, ROUND, M_PASSES, P], U8, align_bytes=64)
+            for t in range(ROUND):
+                e_sb = work.tile([P, L], BF16, bufs=4)
+                nc.scalar.activation(
+                    out=e_sb[:],
+                    in_=a_sb[b][:, h * ROUND + t, :],
+                    func=ACT.Exp,
+                    bias=neg_maxima[r][:, t : t + 1],
+                    scale=1.0,
+                    accum_out=e_sum[:, t : t + 1],
+                )
+                e_words = e_sb[:].bitcast(F32)
+                transpose_pairs(
+                    [e_words[:, n * P : (n + 1) * P] for n in range(4)],
+                    eT_grouped[:, t, :].bitcast(F32).rearrange("q (c l u) -> q c l u", c=M_PASSES, u=2),
+                )
+            quantise(
+                eT_grouped[:].rearrange("q t k -> q (t k)"),
+                eT_codes[:].rearrange("q t c l -> q (t c l)"),
+                eT_scales[:].rearrange("q t c l -> q (t c l)"),
+            )
+
+            e_rsum = work.tile([P, ROUND], F32)
+            nc.vector.reciprocal(out=e_rsum[:], in_=e_sum[:])
+            rsum_bank = psum.tile([P, ROUND, P], F32, tag="rsum_bank")
+            for t in range(ROUND):
+                nc.tensor.transpose(rsum_bank[:, t, :], e_rsum[:, t : t + 1].to_broadcast([P, P]), ident[:])
+            rsum_all = work.tile([P, ROUND, P], F32)
+            nc.scalar.copy(out=rsum_all[:], in_=rsum_bank[:])
+
+            y_grouped = work.tile([P, ROUND, P, PACK], BF16, align_bytes=64)
+            y_codes = work.tile([P, ROUND * P], U32, align_bytes=64)
+            y_scales = work.tile([P, ROUND * P], U8, align_bytes=64)
+            for t in range(ROUND):
+                y_bank = psum.tile([P, F_TILES, P], F32, tag="y_bank", bufs=3)
+                for j in range(F_TILES):
+                    for c in range(M_PASSES):
+                        nc.tensor.matmul_mx(
+                            out=y_bank[:, j, :],
+                            lhsT=gT_codes[:, c, j, :].bitcast(FP8X4),
+                            lhsT_scale=gT_scales[:, c, j, :],
+                            rhs=eT_codes[:, t, c, :].bitcast(FP8X4),
+                            rhs_scale=eT_scales[:, t, c, :],
+                            start=(c == 0),
+                            stop=(c == M_PASSES - 1),
+                        )
+                nc.vector.tensor_tensor(
+                    out=y_grouped[:, t, :, :],
+                    in0=y_bank[:].rearrange("q j l -> q l j"),
+                    in1=rsum_all[:, t, :].unsqueeze(2).to_broadcast([P, P, PACK]),
+                    op=ALU.mult,
+                )
+            quantise(y_grouped[:].rearrange("q t l j -> q (t l j)"), y_codes[:], y_scales[:])
+
+            cols = slice(h * ROUND * P, (h + 1) * ROUND * P)
+            out_bank = psum.tile([P, ROUND * P], F32, tag="out_bank")
+            nc.tensor.matmul_mx(
+                out=out_bank[:],
+                lhsT=w_codes[:, 0, :].bitcast(FP8X4),
+                lhsT_scale=w_scales[:, 0, :],
+                rhs=gp_codes[:, cols].bitcast(FP8X4),
+                rhs_scale=gp_scales[:, cols],
+                start=True,
+                stop=False,
+            )
+            nc.tensor.matmul_mx(
+                out=out_bank[:],
+                lhsT=w_codes[:, 1, :].bitcast(FP8X4),
+                lhsT_scale=w_scales[:, 1, :],
+                rhs=y_codes[:].bitcast(FP8X4),
+                rhs_scale=y_scales[:],
+                start=False,
+                stop=True,
+            )
+            out_sb = work.tile([P, ROUND * P], F32)
+            nc.scalar.activation(out=out_sb[:], in_=out_bank[:], func=ACT.Identity, bias=bias[:, 0:1], scale=1.0)
+            nc.sync.dma_start(out=out[b, :, cols], in_=out_sb[:])

@@ -17,12 +17,17 @@ PACK = 4
 K_PASS = P * PACK
 CLIPS, L, FEAT, CH = 4, 1024, 512, 128
 L_TILES = L // P
+TILES = CLIPS * L_TILES
 M_PASSES = L // K_PASS
 F_TILES = FEAT // P
 ROUND = 4
-ROUNDS = L_TILES // ROUND
-FOLD_STOP = 64
-MAX_AHEAD = 2
+N_ROUNDS = TILES // ROUND
+
+COPY_LAG = 1
+QUANT_LAG = 2
+NORM_LAG = ROUND + 2
+AGG_LAG = NORM_LAG - 1
+LAST_LAG = ROUND - 1 + NORM_LAG + 2
 
 FLOPS = 2 * CLIPS * (L * L * FEAT + 2 * L * FEAT * CH)
 
@@ -33,190 +38,289 @@ def tile_stnonlocalgnlstage_pb_t_kernel(tc, att_logits, g, w1_w, w1_b, w2_w, w2_
         const = stack.enter_context(tc.tile_pool(name="const", bufs=1))
         inputs = stack.enter_context(tc.tile_pool(name="inputs", bufs=1))
         work = stack.enter_context(tc.tile_pool(name="work", bufs=2))
-        psum = stack.enter_context(tc.psum_pool(name="psum", bufs=1))
+        psum = stack.enter_context(tc.psum_pool(name="psum", bufs=2))
+        stack.enter_context(tc.manual_schedule())
 
         a_sb = [inputs.tile([P, L_TILES, L], BF16, name="a%d" % b) for b in range(CLIPS)]
         g_sb = [inputs.tile([P, PACK, L], BF16, name="g%d" % b) for b in range(CLIPS)]
         w_sb = const.tile([P, 2, FEAT], BF16)
         bias_rows = const.tile([P, P], BF16)
 
-        def load_logits(b, h):
-            tiles = slice(h * ROUND, (h + 1) * ROUND)
+        def load_logits(b, first, count):
             rows = att_logits[b].rearrange("(i p) m -> p i m", p=P)
-            nc.sync.dma_start(out=a_sb[b][:, tiles, :], in_=rows[:, tiles, :])
+            nc.sync.dma_start(out=a_sb[b][:, first : first + count, :], in_=rows[:, first : first + count, :])
 
         def load_values(b):
             nc.sync.dma_start(out=g_sb[b][:], in_=g[b].rearrange("(q j) m -> q j m", j=PACK))
 
         nc.gpsimd.memset(bias_rows[:], 0.0)
-        load_logits(0, 0)
-        load_values(0)
         nc.sync.dma_start(out=w_sb[:, 0, :], in_=w1_w)
         nc.sync.dma_start(out=w_sb[:, 1, :], in_=w2_w)
         nc.sync.dma_start(out=bias_rows[0:1, :], in_=w1_b.rearrange("(o c) -> o c", o=1))
         nc.sync.dma_start(out=bias_rows[1:2, :], in_=w2_b.rearrange("(o c) -> o c", o=1))
-        load_logits(0, 1)
+        load_logits(0, 0, 1)
+        load_logits(0, 1, 1)
+        load_values(0)
+        load_logits(0, 2, 1)
+        load_logits(0, 3, 1)
+        load_logits(0, ROUND, ROUND)
         for b in range(1, CLIPS):
             load_values(b)
-            for h in range(ROUNDS):
-                load_logits(b, h)
+            for first in range(0, L_TILES, ROUND):
+                load_logits(b, first, ROUND)
 
         ident = const.tile([P, P], F32)
         make_identity(nc, ident[:])
         ident_bf = const.tile([P, P], BF16)
         make_identity(nc, ident_bf[:])
 
-        def transpose_pairs(blocks, grouped):
-            bank = psum.tile([P, 4, P], F32, tag="bank", bufs=3)
+        def transpose_pairs(blocks, tag):
+            bank = psum.tile([P, 4, P], F32, name=tag, tag=tag)
             for n, block in enumerate(blocks):
                 nc.tensor.transpose(bank[:, n, :], block, ident[:])
+            return bank
+
+        def copy_pairs(bank, grouped):
             nc.scalar.copy(out=grouped, in_=bank[:].rearrange("q (c u) r -> q c r u", u=2))
 
         def quantise(grouped, codes, scales):
             nc.vector.quantize_mx(out=codes.bitcast(FP8X4), scales=scales, in_=grouped)
 
-        def row_maxima(b, h):
-            src = a_sb[b][:, h * ROUND : (h + 1) * ROUND, :]
-            width = L // 2
-            while width >= FOLD_STOP:
-                fold = work.tile([P, ROUND, width], BF16, tag="fold")
-                nc.vector.tensor_tensor(
-                    out=fold[:], in0=src[:, :, 0:width], in1=src[:, :, width : 2 * width], op=ALU.max
-                )
-                src = fold
-                width //= 2
-            neg_max = work.tile([P, ROUND], F32, tag="neg_max", bufs=MAX_AHEAD + 2)
-            nc.vector.tensor_reduce(out=neg_max[:], in_=src[:], axis=AXIS.X, op=ALU.max, negate=True)
-            return neg_max
-
         w_grouped = const.tile([P, 2 * CH * PACK], BF16, align_bytes=64)
         w_codes = const.tile([P, 2, CH], U32, align_bytes=64)
         w_scales = const.tile([P, 2, CH], U8, align_bytes=64)
         w_words = w_sb[:].rearrange("c w p -> c (w p)").bitcast(F32).rearrange("c (w q u) -> c w u q", w=2, u=2)
-        transpose_pairs(
-            [w_words[:, w, u, :] for w in range(2) for u in range(2)],
-            w_grouped[:].bitcast(F32).rearrange("q (w c u) -> q w c u", w=2, u=2),
-        )
-        quantise(
-            w_grouped[:],
-            w_codes[:].rearrange("q w c -> q (w c)"),
-            w_scales[:].rearrange("q w c -> q (w c)"),
-        )
-
-        bias_cols = psum.tile([P, P], BF16, tag="bank", bufs=3)
+        w_bank = transpose_pairs([w_words[:, w, u, :] for w in range(2) for u in range(2)], "g_bank")
+        copy_pairs(w_bank, w_grouped[:].bitcast(F32).rearrange("q (w c u) -> q w c u", w=2, u=2))
+        bias_cols = psum.tile([P, P], BF16, tag="g_bank")
         nc.tensor.transpose(bias_cols[:], bias_rows[:], ident_bf[:])
         bias = const.tile([P, 1], F32)
         nc.vector.tensor_reduce(out=bias[:], in_=bias_cols[:, 0:2], axis=AXIS.X, op=ALU.add)
 
-        rounds = [(b, h) for b in range(CLIPS) for h in range(ROUNDS)]
-        neg_maxima = [row_maxima(b, h) for (b, h) in rounds[:MAX_AHEAD]]
-
-        for r, (b, h) in enumerate(rounds):
-            if r + MAX_AHEAD < len(rounds):
-                neg_maxima.append(row_maxima(*rounds[r + MAX_AHEAD]))
-
-            if h == 0:
-                gT_grouped = work.tile([P, M_PASSES * FEAT * PACK], BF16, align_bytes=64, bufs=1)
-                gT_codes = work.tile([P, M_PASSES, F_TILES, P], U32, align_bytes=64)
-                gT_scales = work.tile([P, M_PASSES, F_TILES, P], U8, align_bytes=64)
-                gT_words = gT_grouped[:].bitcast(F32).rearrange("q (c j f u) -> q c j f u", c=M_PASSES, j=F_TILES, u=2)
-                for j in range(F_TILES):
-                    g_words = g_sb[b][:, j, :].bitcast(F32)
-                    transpose_pairs(
-                        [g_words[:, n * P : (n + 1) * P] for n in range(4)], gT_words[:, :, j, :, :]
-                    )
+        neg_max = {0: work.tile([P, ROUND], F32, name="neg_max")}
+        for t in range(ROUND):
+            nc.vector.tensor_reduce(
+                out=neg_max[0][:, t : t + 1], in_=a_sb[0][:, t, :], axis=AXIS.X, op=ALU.max, negate=True
+            )
+            if t == 1:
                 quantise(
-                    gT_grouped[:],
-                    gT_codes[:].rearrange("q c j f -> q (c j f)"),
-                    gT_scales[:].rearrange("q c j f -> q (c j f)"),
+                    w_grouped[:],
+                    w_codes[:].rearrange("q w c -> q (w c)"),
+                    w_scales[:].rearrange("q w c -> q (w c)"),
                 )
 
-                gp_grouped = work.tile([P, L, PACK], BF16, align_bytes=64, bufs=1)
-                gp_codes = work.tile([P, L], U32, align_bytes=64)
-                gp_scales = work.tile([P, L], U8, align_bytes=64)
-                nc.vector.tensor_copy(
-                    out=gp_grouped[:].rearrange("q (n i) j -> q n j i", i=4),
-                    in_=g_sb[b][:].rearrange("q j (n i) -> q n j i", i=4),
-                )
-                quantise(gp_grouped[:].rearrange("q l j -> q (l j)"), gp_codes[:], gp_scales[:])
+        folded = {}
 
-            e_sum = work.tile([P, ROUND], F32)
-            eT_grouped = work.tile([P, ROUND, M_PASSES * P * PACK], BF16, align_bytes=64)
-            eT_codes = work.tile([P, ROUND, M_PASSES, P], U32, align_bytes=64)
-            eT_scales = work.tile([P, ROUND, M_PASSES, P], U8, align_bytes=64)
-            for t in range(ROUND):
-                e_sb = work.tile([P, L], BF16, bufs=4)
-                nc.scalar.activation(
-                    out=e_sb[:],
-                    in_=a_sb[b][:, h * ROUND + t, :],
-                    func=ACT.Exp,
-                    bias=neg_maxima[r][:, t : t + 1],
-                    scale=1.0,
-                    accum_out=e_sum[:, t : t + 1],
+        def max_step(rho, step):
+            b, first = divmod(rho * ROUND, L_TILES)
+            src = a_sb[b][:, first : first + ROUND, :] if step == 0 else folded[step - 1]
+            width = L >> (step + 1)
+            if step < ROUND - 1:
+                folded[step] = work.tile([P, ROUND, width], BF16, name="fold%d" % step, bufs=1)
+                nc.vector.tensor_tensor(
+                    out=folded[step][:], in0=src[:, :, 0:width], in1=src[:, :, width : 2 * width], op=ALU.max
                 )
-                e_words = e_sb[:].bitcast(F32)
-                transpose_pairs(
-                    [e_words[:, n * P : (n + 1) * P] for n in range(4)],
-                    eT_grouped[:, t, :].bitcast(F32).rearrange("q (c l u) -> q c l u", c=M_PASSES, u=2),
-                )
-            quantise(
-                eT_grouped[:].rearrange("q t k -> q (t k)"),
-                eT_codes[:].rearrange("q t c l -> q (t c l)"),
-                eT_scales[:].rearrange("q t c l -> q (t c l)"),
+            else:
+                neg_max[rho] = work.tile([P, ROUND], F32, name="neg_max")
+                nc.vector.tensor_reduce(out=neg_max[rho][:], in_=src[:], axis=AXIS.X, op=ALU.max, negate=True)
+
+        e_sum, e_sb, e_bank, eT_grouped, eT_codes, eT_scales = {}, {}, {}, {}, {}, {}
+
+        def exponential(k):
+            b, i = divmod(k, L_TILES)
+            r, t = divmod(k, ROUND)
+            if t == 0:
+                e_sum[r] = work.tile([P, ROUND], F32, name="e_sum", bufs=3)
+            e_sb[k] = work.tile([P, L], BF16, name="e_sb", bufs=3)
+            nc.scalar.activation(
+                out=e_sb[k][:],
+                in_=a_sb[b][:, i, :],
+                func=ACT.Exp,
+                bias=neg_max[r][:, t : t + 1],
+                scale=1.0,
+                accum_out=e_sum[r][:, t : t + 1],
             )
 
-            e_rsum = work.tile([P, ROUND], F32)
-            nc.vector.reciprocal(out=e_rsum[:], in_=e_sum[:])
-            rsum_bank = psum.tile([P, ROUND, P], F32, tag="rsum_bank")
-            for t in range(ROUND):
-                nc.tensor.transpose(rsum_bank[:, t, :], e_rsum[:, t : t + 1].to_broadcast([P, P]), ident[:])
-            rsum_all = work.tile([P, ROUND, P], F32)
-            nc.scalar.copy(out=rsum_all[:], in_=rsum_bank[:])
+        def transpose_e(k):
+            e_words = e_sb[k][:].bitcast(F32)
+            e_bank[k] = transpose_pairs([e_words[:, n * P : (n + 1) * P] for n in range(4)], "e_bank")
 
-            y_grouped = work.tile([P, ROUND, P, PACK], BF16, align_bytes=64)
-            y_codes = work.tile([P, ROUND * P], U32, align_bytes=64)
-            y_scales = work.tile([P, ROUND * P], U8, align_bytes=64)
-            for t in range(ROUND):
-                y_bank = psum.tile([P, F_TILES, P], F32, tag="y_bank", bufs=3)
-                for j in range(F_TILES):
-                    for c in range(M_PASSES):
-                        nc.tensor.matmul_mx(
-                            out=y_bank[:, j, :],
-                            lhsT=gT_codes[:, c, j, :].bitcast(FP8X4),
-                            lhsT_scale=gT_scales[:, c, j, :],
-                            rhs=eT_codes[:, t, c, :].bitcast(FP8X4),
-                            rhs_scale=eT_scales[:, t, c, :],
-                            start=(c == 0),
-                            stop=(c == M_PASSES - 1),
-                        )
-                nc.vector.tensor_tensor(
-                    out=y_grouped[:, t, :, :],
-                    in0=y_bank[:].rearrange("q j l -> q l j"),
-                    in1=rsum_all[:, t, :].unsqueeze(2).to_broadcast([P, P, PACK]),
-                    op=ALU.mult,
-                )
-            quantise(y_grouped[:].rearrange("q t l j -> q (t l j)"), y_codes[:], y_scales[:])
+        def copy_e(k):
+            eT_grouped[k] = work.tile([P, M_PASSES * P * PACK], BF16, name="eT_grouped", align_bytes=64, bufs=3)
+            copy_pairs(e_bank[k], eT_grouped[k][:].bitcast(F32).rearrange("q (c l u) -> q c l u", c=M_PASSES, u=2))
 
-            cols = slice(h * ROUND * P, (h + 1) * ROUND * P)
-            out_bank = psum.tile([P, ROUND * P], F32, tag="out_bank")
+        def quantise_e(k):
+            eT_codes[k] = work.tile([P, M_PASSES, P], U32, name="eT_codes", align_bytes=64, bufs=AGG_LAG)
+            eT_scales[k] = work.tile([P, M_PASSES, P], U8, name="eT_scales", align_bytes=64, bufs=AGG_LAG)
+            quantise(
+                eT_grouped[k][:],
+                eT_codes[k][:].rearrange("q c l -> q (c l)"),
+                eT_scales[k][:].rearrange("q c l -> q (c l)"),
+            )
+
+        g_bank, gT_grouped, gT_codes, gT_scales, gp_grouped, gp_codes, gp_scales = {}, {}, {}, {}, {}, {}, {}
+
+        def transpose_g(b, j):
+            g_words = g_sb[b][:, j, :].bitcast(F32)
+            g_bank[j] = transpose_pairs([g_words[:, n * P : (n + 1) * P] for n in range(4)], "g_bank")
+
+        def copy_g(b, j):
+            if j == 0:
+                gT_grouped[b] = work.tile([P, M_PASSES * FEAT * PACK], BF16, name="gT_grouped", align_bytes=64, bufs=1)
+            gT_words = gT_grouped[b][:].bitcast(F32).rearrange("q (c j f u) -> q c j f u", c=M_PASSES, j=F_TILES, u=2)
+            copy_pairs(g_bank[j], gT_words[:, :, j, :, :])
+
+        def quantise_gT(b):
+            gT_codes[b] = work.tile([P, M_PASSES, F_TILES, P], U32, name="gT_codes", align_bytes=64)
+            gT_scales[b] = work.tile([P, M_PASSES, F_TILES, P], U8, name="gT_scales", align_bytes=64)
+            quantise(
+                gT_grouped[b][:],
+                gT_codes[b][:].rearrange("q c j f -> q (c j f)"),
+                gT_scales[b][:].rearrange("q c j f -> q (c j f)"),
+            )
+
+        def regroup_g(b, quarter):
+            if quarter == 0:
+                gp_grouped[b] = work.tile([P, L, PACK], BF16, name="gp_grouped", align_bytes=64, bufs=1)
+            cols = slice(quarter * L // 4, (quarter + 1) * L // 4)
+            nc.vector.tensor_copy(
+                out=gp_grouped[b][:, cols, :].rearrange("q (n i) j -> q n j i", i=4),
+                in_=g_sb[b][:, :, cols].rearrange("q j (n i) -> q n j i", i=4),
+            )
+
+        def quantise_gp(b):
+            gp_codes[b] = work.tile([P, L], U32, name="gp_codes", align_bytes=64)
+            gp_scales[b] = work.tile([P, L], U8, name="gp_scales", align_bytes=64)
+            quantise(gp_grouped[b][:].rearrange("q l j -> q (l j)"), gp_codes[b][:], gp_scales[b][:])
+
+        e_rsum, rsum_bank, rsum_all = {}, {}, {}
+
+        def reciprocal_sums(r):
+            e_rsum[r] = work.tile([P, ROUND], F32, name="e_rsum")
+            nc.vector.reciprocal(out=e_rsum[r][:], in_=e_sum[r][:])
+
+        def spread_sums(r):
+            rsum_bank[r] = psum.tile([P, ROUND, P], F32, name="rsum_bank", bufs=1)
+            for t in range(ROUND):
+                nc.tensor.transpose(rsum_bank[r][:, t, :], e_rsum[r][:, t : t + 1].to_broadcast([P, P]), ident[:])
+
+        def copy_sums(r):
+            rsum_all[r] = work.tile([P, ROUND, P], F32, name="rsum_all")
+            nc.scalar.copy(out=rsum_all[r][:], in_=rsum_bank[r][:])
+
+        y_bank, y_grouped, y_codes, y_scales, out_bank = {}, {}, {}, {}, {}
+
+        def aggregate(k):
+            b = k // L_TILES
+            y_bank[k] = psum.tile([P, F_TILES, P], F32, name="y_bank")
+            for j in range(F_TILES):
+                for c in range(M_PASSES):
+                    nc.tensor.matmul_mx(
+                        out=y_bank[k][:, j, :],
+                        lhsT=gT_codes[b][:, c, j, :].bitcast(FP8X4),
+                        lhsT_scale=gT_scales[b][:, c, j, :],
+                        rhs=eT_codes[k][:, c, :].bitcast(FP8X4),
+                        rhs_scale=eT_scales[k][:, c, :],
+                        start=(c == 0),
+                        stop=(c == M_PASSES - 1),
+                    )
+
+        def normalise(k):
+            r, t = divmod(k, ROUND)
+            if t == 0:
+                y_grouped[r] = work.tile([P, ROUND, P, PACK], BF16, name="y_grouped", align_bytes=64)
+            nc.vector.tensor_tensor(
+                out=y_grouped[r][:, t, :, :],
+                in0=y_bank[k][:].rearrange("q j l -> q l j"),
+                in1=rsum_all[r][:, t, :].unsqueeze(2).to_broadcast([P, P, PACK]),
+                op=ALU.mult,
+            )
+
+        def quantise_y(r):
+            y_codes[r] = work.tile([P, ROUND * P], U32, name="y_codes", align_bytes=64)
+            y_scales[r] = work.tile([P, ROUND * P], U8, name="y_scales", align_bytes=64)
+            quantise(y_grouped[r][:].rearrange("q t l j -> q (t l j)"), y_codes[r][:], y_scales[r][:])
+
+        def project(r):
+            b, first = divmod(r * ROUND, L_TILES)
+            cols = slice(first * P, (first + ROUND) * P)
+            out_bank[r] = psum.tile([P, ROUND * P], F32, name="out_bank", bufs=1)
             nc.tensor.matmul_mx(
-                out=out_bank[:],
+                out=out_bank[r][:],
                 lhsT=w_codes[:, 0, :].bitcast(FP8X4),
                 lhsT_scale=w_scales[:, 0, :],
-                rhs=gp_codes[:, cols].bitcast(FP8X4),
-                rhs_scale=gp_scales[:, cols],
+                rhs=gp_codes[b][:, cols].bitcast(FP8X4),
+                rhs_scale=gp_scales[b][:, cols],
                 start=True,
                 stop=False,
             )
             nc.tensor.matmul_mx(
-                out=out_bank[:],
+                out=out_bank[r][:],
                 lhsT=w_codes[:, 1, :].bitcast(FP8X4),
                 lhsT_scale=w_scales[:, 1, :],
-                rhs=y_codes[:].bitcast(FP8X4),
-                rhs_scale=y_scales[:],
+                rhs=y_codes[r][:].bitcast(FP8X4),
+                rhs_scale=y_scales[r][:],
                 start=False,
                 stop=True,
             )
+
+        def store(r):
+            b, first = divmod(r * ROUND, L_TILES)
             out_sb = work.tile([P, ROUND * P], F32)
-            nc.scalar.activation(out=out_sb[:], in_=out_bank[:], func=ACT.Identity, bias=bias[:, 0:1], scale=1.0)
-            nc.sync.dma_start(out=out[b, :, cols], in_=out_sb[:])
+            nc.scalar.activation(out=out_sb[:], in_=out_bank[r][:], func=ACT.Identity, bias=bias[:, 0:1], scale=1.0)
+            nc.sync.dma_start(out=out[b, :, first * P : (first + ROUND) * P], in_=out_sb[:])
+
+        def tile_due(k):
+            return 0 <= k < TILES
+
+        def round_due(tick):
+            r, t = divmod(tick, ROUND)
+            return r if t == 0 and 0 <= r < N_ROUNDS else None
+
+        def clip_piece_due(tick):
+            b, i = divmod(tick, L_TILES)
+            return (b, i) if 0 <= b < CLIPS and i < F_TILES else None
+
+        def clip_due(tick):
+            b, i = divmod(tick, L_TILES)
+            return b if i == 0 and 0 <= b < CLIPS else None
+
+        for k in range(N_ROUNDS * ROUND - ROUND + LAST_LAG + 1):
+            if tile_due(k):
+                exponential(k)
+            if tile_due(k - COPY_LAG):
+                copy_e(k - COPY_LAG)
+            if round_due(k - ROUND - 1) is not None:
+                copy_sums(round_due(k - ROUND - 1))
+            if clip_piece_due(k - 1) is not None:
+                copy_g(*clip_piece_due(k - 1))
+            if round_due(k - LAST_LAG) is not None:
+                store(round_due(k - LAST_LAG))
+
+            if round_due(k - ROUND) is not None:
+                reciprocal_sums(round_due(k - ROUND))
+            if clip_due(k - AGG_LAG) is not None:
+                quantise_gT(clip_due(k - AGG_LAG))
+            if tile_due(k - NORM_LAG):
+                normalise(k - NORM_LAG)
+            if tile_due(k - QUANT_LAG):
+                quantise_e(k - QUANT_LAG)
+            if k // ROUND + 1 < N_ROUNDS:
+                max_step(k // ROUND + 1, k % ROUND)
+            if clip_piece_due(k - 1) is not None:
+                regroup_g(*clip_piece_due(k - 1))
+            if round_due(k - LAST_LAG + 2) is not None:
+                quantise_y(round_due(k - LAST_LAG + 2))
+            if clip_due(k - AGG_LAG - 1) is not None:
+                quantise_gp(clip_due(k - AGG_LAG - 1))
+
+            if tile_due(k - AGG_LAG):
+                aggregate(k - AGG_LAG)
+            if round_due(k - LAST_LAG + 1) is not None:
+                project(round_due(k - LAST_LAG + 1))
+            if round_due(k - ROUND) is not None:
+                spread_sums(round_due(k - ROUND))
+            if tile_due(k):
+                transpose_e(k)
+            if clip_piece_due(k) is not None:
+                transpose_g(*clip_piece_due(k))

@@ -22,11 +22,14 @@ M_PASSES = L // K_PASS
 F_TILES = FEAT // P
 ROUND = 4
 N_ROUNDS = TILES // ROUND
+PAIR = 2
+N_PAIRS = TILES // PAIR
 
 COPY_LAG = 1
 QUANT_LAG = 2
-NORM_LAG = ROUND + 2
-AGG_LAG = NORM_LAG - 1
+AGG_LAG = 4
+NORM_LAG = AGG_LAG + 1
+MAX_LEAD = 1
 LAST_LAG = ROUND - 1 + NORM_LAG + 2
 
 FLOPS = 2 * CLIPS * (L * L * FEAT + 2 * L * FEAT * CH)
@@ -129,8 +132,9 @@ def tile_stnonlocalgnlstage_pb_t_kernel(tc, att_logits, g, w1_w, w1_b, w2_w, w2_
         def exponential(k):
             b, i = divmod(k, L_TILES)
             r, t = divmod(k, ROUND)
-            if t == 0:
-                e_sum[r] = work.tile([P, ROUND], F32, name="e_sum", bufs=3)
+            h, s = divmod(k, PAIR)
+            if s == 0:
+                e_sum[h] = work.tile([P, PAIR], F32, name="e_sum", bufs=3)
             e_sb[k] = work.tile([P, L], BF16, name="e_sb", bufs=3)
             nc.scalar.activation(
                 out=e_sb[k][:],
@@ -138,7 +142,7 @@ def tile_stnonlocalgnlstage_pb_t_kernel(tc, att_logits, g, w1_w, w1_b, w2_w, w2_
                 func=ACT.Exp,
                 bias=neg_max[r][:, t : t + 1],
                 scale=1.0,
-                accum_out=e_sum[r][:, t : t + 1],
+                accum_out=e_sum[h][:, s : s + 1],
             )
 
         def transpose_e(k):
@@ -150,8 +154,8 @@ def tile_stnonlocalgnlstage_pb_t_kernel(tc, att_logits, g, w1_w, w1_b, w2_w, w2_
             copy_pairs(e_bank[k], eT_grouped[k][:].bitcast(F32).rearrange("q (c l u) -> q c l u", c=M_PASSES, u=2))
 
         def quantise_e(k):
-            eT_codes[k] = work.tile([P, M_PASSES, P], U32, name="eT_codes", align_bytes=64, bufs=AGG_LAG)
-            eT_scales[k] = work.tile([P, M_PASSES, P], U8, name="eT_scales", align_bytes=64, bufs=AGG_LAG)
+            eT_codes[k] = work.tile([P, M_PASSES, P], U32, name="eT_codes", align_bytes=64, bufs=4)
+            eT_scales[k] = work.tile([P, M_PASSES, P], U8, name="eT_scales", align_bytes=64, bufs=4)
             quantise(
                 eT_grouped[k][:],
                 eT_codes[k][:].rearrange("q c l -> q (c l)"),
@@ -179,10 +183,10 @@ def tile_stnonlocalgnlstage_pb_t_kernel(tc, att_logits, g, w1_w, w1_b, w2_w, w2_
                 gT_scales[b][:].rearrange("q c j f -> q (c j f)"),
             )
 
-        def regroup_g(b, quarter):
-            if quarter == 0:
+        def regroup_g(b, half):
+            if half == 0:
                 gp_grouped[b] = work.tile([P, L, PACK], BF16, name="gp_grouped", align_bytes=64, bufs=1)
-            cols = slice(quarter * L // 4, (quarter + 1) * L // 4)
+            cols = slice(half * L // 2, (half + 1) * L // 2)
             nc.vector.tensor_copy(
                 out=gp_grouped[b][:, cols, :].rearrange("q (n i) j -> q n j i", i=4),
                 in_=g_sb[b][:, :, cols].rearrange("q j (n i) -> q n j i", i=4),
@@ -195,18 +199,18 @@ def tile_stnonlocalgnlstage_pb_t_kernel(tc, att_logits, g, w1_w, w1_b, w2_w, w2_
 
         e_rsum, rsum_bank, rsum_all = {}, {}, {}
 
-        def reciprocal_sums(r):
-            e_rsum[r] = work.tile([P, ROUND], F32, name="e_rsum")
-            nc.vector.reciprocal(out=e_rsum[r][:], in_=e_sum[r][:])
+        def reciprocal_sums(h):
+            e_rsum[h] = work.tile([P, PAIR], F32, name="e_rsum")
+            nc.vector.reciprocal(out=e_rsum[h][:], in_=e_sum[h][:])
 
-        def spread_sums(r):
-            rsum_bank[r] = psum.tile([P, ROUND, P], F32, name="rsum_bank", bufs=1)
-            for t in range(ROUND):
-                nc.tensor.transpose(rsum_bank[r][:, t, :], e_rsum[r][:, t : t + 1].to_broadcast([P, P]), ident[:])
+        def spread_sums(h):
+            rsum_bank[h] = psum.tile([P, PAIR, P], F32, name="rsum_bank", bufs=1)
+            for s in range(PAIR):
+                nc.tensor.transpose(rsum_bank[h][:, s, :], e_rsum[h][:, s : s + 1].to_broadcast([P, P]), ident[:])
 
-        def copy_sums(r):
-            rsum_all[r] = work.tile([P, ROUND, P], F32, name="rsum_all")
-            nc.scalar.copy(out=rsum_all[r][:], in_=rsum_bank[r][:])
+        def copy_sums(h):
+            rsum_all[h] = work.tile([P, PAIR, P], F32, name="rsum_all", bufs=3)
+            nc.scalar.copy(out=rsum_all[h][:], in_=rsum_bank[h][:])
 
         y_bank, y_grouped, y_codes, y_scales, out_bank = {}, {}, {}, {}, {}
 
@@ -227,12 +231,13 @@ def tile_stnonlocalgnlstage_pb_t_kernel(tc, att_logits, g, w1_w, w1_b, w2_w, w2_
 
         def normalise(k):
             r, t = divmod(k, ROUND)
+            h, s = divmod(k, PAIR)
             if t == 0:
                 y_grouped[r] = work.tile([P, ROUND, P, PACK], BF16, name="y_grouped", align_bytes=64)
             nc.vector.tensor_tensor(
                 out=y_grouped[r][:, t, :, :],
                 in0=y_bank[k][:].rearrange("q j l -> q l j"),
-                in1=rsum_all[r][:, t, :].unsqueeze(2).to_broadcast([P, P, PACK]),
+                in1=rsum_all[h][:, s, :].unsqueeze(2).to_broadcast([P, P, PACK]),
                 op=ALU.mult,
             )
 
@@ -277,38 +282,44 @@ def tile_stnonlocalgnlstage_pb_t_kernel(tc, att_logits, g, w1_w, w1_b, w2_w, w2_
             r, t = divmod(tick, ROUND)
             return r if t == 0 and 0 <= r < N_ROUNDS else None
 
-        def clip_piece_due(tick):
+        def pair_due(tick):
+            h, s = divmod(tick, PAIR)
+            return h if s == 0 and 0 <= h < N_PAIRS else None
+
+        def clip_half_due(tick):
             b, i = divmod(tick, L_TILES)
-            return (b, i) if 0 <= b < CLIPS and i < F_TILES else None
+            return (b, i) if 0 <= b < CLIPS and i < 2 else None
 
         def clip_due(tick):
             b, i = divmod(tick, L_TILES)
             return b if i == 0 and 0 <= b < CLIPS else None
 
-        for k in range(N_ROUNDS * ROUND - ROUND + LAST_LAG + 1):
+        for k in range(-MAX_LEAD, N_ROUNDS * ROUND - ROUND + LAST_LAG + 1):
             if tile_due(k):
                 exponential(k)
             if tile_due(k - COPY_LAG):
                 copy_e(k - COPY_LAG)
-            if round_due(k - ROUND - 1) is not None:
-                copy_sums(round_due(k - ROUND - 1))
-            if clip_piece_due(k - 1) is not None:
-                copy_g(*clip_piece_due(k - 1))
+            if pair_due(k - PAIR - 1) is not None:
+                copy_sums(pair_due(k - PAIR - 1))
+            if clip_half_due(k - 1) is not None:
+                b, half = clip_half_due(k - 1)
+                copy_g(b, 2 * half)
+                copy_g(b, 2 * half + 1)
             if round_due(k - LAST_LAG) is not None:
                 store(round_due(k - LAST_LAG))
 
-            if round_due(k - ROUND) is not None:
-                reciprocal_sums(round_due(k - ROUND))
+            if pair_due(k - PAIR) is not None:
+                reciprocal_sums(pair_due(k - PAIR))
             if clip_due(k - AGG_LAG) is not None:
                 quantise_gT(clip_due(k - AGG_LAG))
             if tile_due(k - NORM_LAG):
                 normalise(k - NORM_LAG)
             if tile_due(k - QUANT_LAG):
                 quantise_e(k - QUANT_LAG)
-            if k // ROUND + 1 < N_ROUNDS:
-                max_step(k // ROUND + 1, k % ROUND)
-            if clip_piece_due(k - 1) is not None:
-                regroup_g(*clip_piece_due(k - 1))
+            if (k + MAX_LEAD) // ROUND + 1 < N_ROUNDS:
+                max_step((k + MAX_LEAD) // ROUND + 1, (k + MAX_LEAD) % ROUND)
+            if clip_half_due(k - 1) is not None:
+                regroup_g(*clip_half_due(k - 1))
             if round_due(k - LAST_LAG + 2) is not None:
                 quantise_y(round_due(k - LAST_LAG + 2))
             if clip_due(k - AGG_LAG - 1) is not None:
@@ -318,9 +329,11 @@ def tile_stnonlocalgnlstage_pb_t_kernel(tc, att_logits, g, w1_w, w1_b, w2_w, w2_
                 aggregate(k - AGG_LAG)
             if round_due(k - LAST_LAG + 1) is not None:
                 project(round_due(k - LAST_LAG + 1))
-            if round_due(k - ROUND) is not None:
-                spread_sums(round_due(k - ROUND))
+            if pair_due(k - PAIR) is not None:
+                spread_sums(pair_due(k - PAIR))
             if tile_due(k):
                 transpose_e(k)
-            if clip_piece_due(k) is not None:
-                transpose_g(*clip_piece_due(k))
+            if clip_half_due(k) is not None:
+                b, half = clip_half_due(k)
+                transpose_g(b, 2 * half)
+                transpose_g(b, 2 * half + 1)

@@ -42,7 +42,6 @@ def tile_stnonlocalgnlstage_pb_t_kernel(tc, att_logits, g, w1_w, w1_b, w2_w, w2_
         inputs = stack.enter_context(tc.tile_pool(name="inputs", bufs=1))
         work = stack.enter_context(tc.tile_pool(name="work", bufs=2))
         psum = stack.enter_context(tc.psum_pool(name="psum", bufs=2))
-        stack.enter_context(tc.manual_schedule())
 
         a_sb = [inputs.tile([P, L_TILES, L], BF16, name="a%d" % b) for b in range(CLIPS)]
         g_sb = [inputs.tile([P, PACK, L], BF16, name="g%d" % b) for b in range(CLIPS)]

@@ -25,12 +25,14 @@ N_ROUNDS = TILES // ROUND
 PAIR = 2
 N_PAIRS = TILES // PAIR
 
+MAX_LEAD = 2
 COPY_LAG = 1
 QUANT_LAG = 2
-AGG_LAG = 4
-NORM_LAG = AGG_LAG + 1
-MAX_LEAD = 1
-LAST_LAG = ROUND - 1 + NORM_LAG + 2
+AGG_LAG = 2
+NORM_LAG = 3
+GP_LAG = 2
+Y_LAG = ROUND - 1 + NORM_LAG
+WEIGHT_TICK = 4
 
 FLOPS = 2 * CLIPS * (L * L * FEAT + 2 * L * FEAT * CH)
 
@@ -42,6 +44,7 @@ def tile_stnonlocalgnlstage_pb_t_kernel(tc, att_logits, g, w1_w, w1_b, w2_w, w2_
         inputs = stack.enter_context(tc.tile_pool(name="inputs", bufs=1))
         work = stack.enter_context(tc.tile_pool(name="work", bufs=2))
         psum = stack.enter_context(tc.psum_pool(name="psum", bufs=2))
+        stack.enter_context(tc.manual_schedule())
 
         a_sb = [inputs.tile([P, L_TILES, L], BF16, name="a%d" % b) for b in range(CLIPS)]
         g_sb = [inputs.tile([P, PACK, L], BF16, name="g%d" % b) for b in range(CLIPS)]
@@ -52,24 +55,30 @@ def tile_stnonlocalgnlstage_pb_t_kernel(tc, att_logits, g, w1_w, w1_b, w2_w, w2_
             rows = att_logits[b].rearrange("(i p) m -> p i m", p=P)
             nc.sync.dma_start(out=a_sb[b][:, first : first + count, :], in_=rows[:, first : first + count, :])
 
-        def load_values(b):
-            nc.sync.dma_start(out=g_sb[b][:], in_=g[b].rearrange("(q j) m -> q j m", j=PACK))
+        def load_values(b, first=0, count=PACK):
+            rows = g[b].rearrange("(q j) m -> q j m", j=PACK)
+            nc.sync.dma_start(out=g_sb[b][:, first : first + count, :], in_=rows[:, first : first + count, :])
 
         nc.gpsimd.memset(bias_rows[:], 0.0)
+        for i in range(3):
+            load_logits(0, i, 1)
+        load_values(0, 0, 2)
+        load_logits(0, 3, 1)
+        load_values(0, 2, 2)
+        load_logits(0, 4, 2)
+        load_logits(0, 6, 2)
         nc.sync.dma_start(out=w_sb[:, 0, :], in_=w1_w)
         nc.sync.dma_start(out=w_sb[:, 1, :], in_=w2_w)
         nc.sync.dma_start(out=bias_rows[0:1, :], in_=w1_b.rearrange("(o c) -> o c", o=1))
         nc.sync.dma_start(out=bias_rows[1:2, :], in_=w2_b.rearrange("(o c) -> o c", o=1))
-        load_logits(0, 0, 1)
-        load_logits(0, 1, 1)
-        load_values(0)
-        load_logits(0, 2, 1)
-        load_logits(0, 3, 1)
-        load_logits(0, ROUND, ROUND)
         for b in range(1, CLIPS):
             load_values(b)
             for first in range(0, L_TILES, ROUND):
                 load_logits(b, first, ROUND)
+
+        warm = const.tile([P, 1], F32)
+        nc.gpsimd.memset(warm[:], 0.0)
+        nc.scalar.activation(out=warm[:], in_=warm[:], func=ACT.Exp)
 
         ident = const.tile([P, P], F32)
         make_identity(nc, ident[:])
@@ -82,8 +91,8 @@ def tile_stnonlocalgnlstage_pb_t_kernel(tc, att_logits, g, w1_w, w1_b, w2_w, w2_
                 nc.tensor.transpose(bank[:, n, :], block, ident[:])
             return bank
 
-        def copy_pairs(bank, grouped):
-            nc.scalar.copy(out=grouped, in_=bank[:].rearrange("q (c u) r -> q c r u", u=2))
+        def copy_pairs(bank, grouped, copy=nc.scalar.copy):
+            copy(out=grouped, in_=bank[:].rearrange("q (c u) r -> q c r u", u=2))
 
         def quantise(grouped, codes, scales):
             nc.vector.quantize_mx(out=codes.bitcast(FP8X4), scales=scales, in_=grouped)
@@ -92,45 +101,47 @@ def tile_stnonlocalgnlstage_pb_t_kernel(tc, att_logits, g, w1_w, w1_b, w2_w, w2_
         w_codes = const.tile([P, 2, CH], U32, align_bytes=64)
         w_scales = const.tile([P, 2, CH], U8, align_bytes=64)
         w_words = w_sb[:].rearrange("c w p -> c (w p)").bitcast(F32).rearrange("c (w q u) -> c w u q", w=2, u=2)
-        w_bank = transpose_pairs([w_words[:, w, u, :] for w in range(2) for u in range(2)], "g_bank")
-        copy_pairs(w_bank, w_grouped[:].bitcast(F32).rearrange("q (w c u) -> q w c u", w=2, u=2))
-        bias_cols = psum.tile([P, P], BF16, tag="g_bank")
-        nc.tensor.transpose(bias_cols[:], bias_rows[:], ident_bf[:])
         bias = const.tile([P, 1], F32)
-        nc.vector.tensor_reduce(out=bias[:], in_=bias_cols[:, 0:2], axis=AXIS.X, op=ALU.add)
+        w_bank, bias_cols = {}, {}
 
-        neg_max = {0: work.tile([P, ROUND], F32, name="neg_max")}
-        for t in range(ROUND):
-            nc.vector.tensor_reduce(
-                out=neg_max[0][:, t : t + 1], in_=a_sb[0][:, t, :], axis=AXIS.X, op=ALU.max, negate=True
+        def transpose_weights():
+            w_bank[0] = transpose_pairs([w_words[:, w, u, :] for w in range(2) for u in range(2)], "g_bank")
+            bias_cols[0] = psum.tile([P, P], BF16, name="bias_cols", tag="g_bank")
+            nc.tensor.transpose(bias_cols[0][:], bias_rows[:], ident_bf[:])
+
+        def copy_weights():
+            copy_pairs(w_bank[0], w_grouped[:].bitcast(F32).rearrange("q (w c u) -> q w c u", w=2, u=2))
+
+        def add_biases():
+            nc.vector.tensor_reduce(out=bias[:], in_=bias_cols[0][:, 0:2], axis=AXIS.X, op=ALU.add)
+
+        def quantise_weights():
+            quantise(
+                w_grouped[:],
+                w_codes[:].rearrange("q w c -> q (w c)"),
+                w_scales[:].rearrange("q w c -> q (w c)"),
             )
-            if t == 1:
-                quantise(
-                    w_grouped[:],
-                    w_codes[:].rearrange("q w c -> q (w c)"),
-                    w_scales[:].rearrange("q w c -> q (w c)"),
-                )
 
-        folded = {}
+        neg_max = {}
 
-        def max_step(rho, step):
-            b, first = divmod(rho * ROUND, L_TILES)
-            src = a_sb[b][:, first : first + ROUND, :] if step == 0 else folded[step - 1]
-            width = L >> (step + 1)
-            if step < ROUND - 1:
-                folded[step] = work.tile([P, ROUND, width], BF16, name="fold%d" % step, bufs=1)
-                nc.vector.tensor_tensor(
-                    out=folded[step][:], in0=src[:, :, 0:width], in1=src[:, :, width : 2 * width], op=ALU.max
-                )
-            else:
-                neg_max[rho] = work.tile([P, ROUND], F32, name="neg_max")
-                nc.vector.tensor_reduce(out=neg_max[rho][:], in_=src[:], axis=AXIS.X, op=ALU.max, negate=True)
+        def maxima(k):
+            b, i = divmod(k, L_TILES)
+            negated = work.tile([P, L], BF16, name="negated")
+            neg_max[k] = work.tile([P, 1], F32, name="neg_max", bufs=MAX_LEAD + 2)
+            nc.vector.tensor_scalar(
+                out=negated[:],
+                in0=a_sb[b][:, i, :],
+                scalar1=-1.0,
+                scalar2=None,
+                op0=ALU.mult,
+                op1=ALU.min,
+                accum_out=neg_max[k][:],
+            )
 
         e_sum, e_sb, e_bank, eT_grouped, eT_codes, eT_scales = {}, {}, {}, {}, {}, {}
 
         def exponential(k):
             b, i = divmod(k, L_TILES)
-            r, t = divmod(k, ROUND)
             h, s = divmod(k, PAIR)
             if s == 0:
                 e_sum[h] = work.tile([P, PAIR], F32, name="e_sum", bufs=3)
@@ -139,7 +150,7 @@ def tile_stnonlocalgnlstage_pb_t_kernel(tc, att_logits, g, w1_w, w1_b, w2_w, w2_
                 out=e_sb[k][:],
                 in_=a_sb[b][:, i, :],
                 func=ACT.Exp,
-                bias=neg_max[r][:, t : t + 1],
+                bias=neg_max[k][:],
                 scale=1.0,
                 accum_out=e_sum[h][:, s : s + 1],
             )
@@ -170,31 +181,39 @@ def tile_stnonlocalgnlstage_pb_t_kernel(tc, att_logits, g, w1_w, w1_b, w2_w, w2_
         def copy_g(b, j):
             if j == 0:
                 gT_grouped[b] = work.tile([P, M_PASSES * FEAT * PACK], BF16, name="gT_grouped", align_bytes=64, bufs=1)
-            gT_words = gT_grouped[b][:].bitcast(F32).rearrange("q (c j f u) -> q c j f u", c=M_PASSES, j=F_TILES, u=2)
-            copy_pairs(g_bank[j], gT_words[:, :, j, :, :])
+            gT_words = gT_grouped[b][:].bitcast(F32).rearrange("q (j c f u) -> q j c f u", c=M_PASSES, j=F_TILES, u=2)
+            copy_pairs(g_bank[j], gT_words[:, j, :, :, :], nc.vector.tensor_copy if b == 0 else nc.scalar.copy)
 
-        def quantise_gT(b):
-            gT_codes[b] = work.tile([P, M_PASSES, F_TILES, P], U32, name="gT_codes", align_bytes=64)
-            gT_scales[b] = work.tile([P, M_PASSES, F_TILES, P], U8, name="gT_scales", align_bytes=64)
+        def quantise_gT(b, j):
+            if j == 0:
+                gT_codes[b] = work.tile([P, F_TILES, M_PASSES, P], U32, name="gT_codes", align_bytes=64)
+                gT_scales[b] = work.tile([P, F_TILES, M_PASSES, P], U8, name="gT_scales", align_bytes=64)
+            width = M_PASSES * P * PACK
             quantise(
-                gT_grouped[b][:],
-                gT_codes[b][:].rearrange("q c j f -> q (c j f)"),
-                gT_scales[b][:].rearrange("q c j f -> q (c j f)"),
+                gT_grouped[b][:, j * width : (j + 1) * width],
+                gT_codes[b][:, j, :, :].rearrange("q c f -> q (c f)"),
+                gT_scales[b][:, j, :, :].rearrange("q c f -> q (c f)"),
             )
 
-        def regroup_g(b, half):
-            if half == 0:
-                gp_grouped[b] = work.tile([P, L, PACK], BF16, name="gp_grouped", align_bytes=64, bufs=1)
-            cols = slice(half * L // 2, (half + 1) * L // 2)
-            nc.vector.tensor_copy(
-                out=gp_grouped[b][:, cols, :].rearrange("q (n i) j -> q n j i", i=4),
-                in_=g_sb[b][:, :, cols].rearrange("q j (n i) -> q n j i", i=4),
+        def regroup_g(k):
+            b, i = divmod(k, L_TILES)
+            gp_grouped[k] = work.tile([P, P, PACK], BF16, name="gp_grouped", align_bytes=64)
+            nc.gpsimd.tensor_scalar(
+                out=gp_grouped[k][:],
+                in0=g_sb[b][:, :, i * P : (i + 1) * P].rearrange("q j l -> q l j"),
+                scalar1=1.0,
+                scalar2=0.0,
+                op0=ALU.mult,
+                op1=ALU.add,
             )
 
-        def quantise_gp(b):
-            gp_codes[b] = work.tile([P, L], U32, name="gp_codes", align_bytes=64)
-            gp_scales[b] = work.tile([P, L], U8, name="gp_scales", align_bytes=64)
-            quantise(gp_grouped[b][:].rearrange("q l j -> q (l j)"), gp_codes[b][:], gp_scales[b][:])
+        def quantise_gp(k):
+            b, i = divmod(k, L_TILES)
+            if i == 0:
+                gp_codes[b] = work.tile([P, L], U32, name="gp_codes", align_bytes=64)
+                gp_scales[b] = work.tile([P, L], U8, name="gp_scales", align_bytes=64)
+            cols = slice(i * P, (i + 1) * P)
+            quantise(gp_grouped[k][:].rearrange("q l j -> q (l j)"), gp_codes[b][:, cols], gp_scales[b][:, cols])
 
         e_rsum, rsum_bank, rsum_all = {}, {}, {}
 
@@ -209,7 +228,7 @@ def tile_stnonlocalgnlstage_pb_t_kernel(tc, att_logits, g, w1_w, w1_b, w2_w, w2_
 
         def copy_sums(h):
             rsum_all[h] = work.tile([P, PAIR, P], F32, name="rsum_all", bufs=3)
-            nc.scalar.copy(out=rsum_all[h][:], in_=rsum_bank[h][:])
+            nc.vector.tensor_copy(out=rsum_all[h][:], in_=rsum_bank[h][:])
 
         y_bank, y_grouped, y_codes, y_scales, out_bank = {}, {}, {}, {}, {}
 
@@ -220,8 +239,8 @@ def tile_stnonlocalgnlstage_pb_t_kernel(tc, att_logits, g, w1_w, w1_b, w2_w, w2_
                 for c in range(M_PASSES):
                     nc.tensor.matmul_mx(
                         out=y_bank[k][:, j, :],
-                        lhsT=gT_codes[b][:, c, j, :].bitcast(FP8X4),
-                        lhsT_scale=gT_scales[b][:, c, j, :],
+                        lhsT=gT_codes[b][:, j, c, :].bitcast(FP8X4),
+                        lhsT_scale=gT_scales[b][:, j, c, :],
                         rhs=eT_codes[k][:, c, :].bitcast(FP8X4),
                         rhs_scale=eT_scales[k][:, c, :],
                         start=(c == 0),
@@ -285,54 +304,68 @@ def tile_stnonlocalgnlstage_pb_t_kernel(tc, att_logits, g, w1_w, w1_b, w2_w, w2_
             h, s = divmod(tick, PAIR)
             return h if s == 0 and 0 <= h < N_PAIRS else None
 
-        def clip_half_due(tick):
-            b, i = divmod(tick, L_TILES)
-            return (b, i) if 0 <= b < CLIPS and i < 2 else None
-
         def clip_due(tick):
             b, i = divmod(tick, L_TILES)
             return b if i == 0 and 0 <= b < CLIPS else None
 
-        for k in range(-MAX_LEAD, N_ROUNDS * ROUND - ROUND + LAST_LAG + 1):
+        def g_tiles_due(tick):
+            if 0 <= tick < F_TILES // 2:
+                return [(0, 2 * tick), (0, 2 * tick + 1)]
+            b, j = divmod(tick + F_TILES, L_TILES)
+            return [(b, j)] if 1 <= b < CLIPS and j < F_TILES else []
+
+        for k in range(-MAX_LEAD, TILES - ROUND + Y_LAG + 3):
             if tile_due(k):
                 exponential(k)
             if tile_due(k - COPY_LAG):
                 copy_e(k - COPY_LAG)
-            if pair_due(k - PAIR - 1) is not None:
-                copy_sums(pair_due(k - PAIR - 1))
-            if clip_half_due(k - 1) is not None:
-                b, half = clip_half_due(k - 1)
-                copy_g(b, 2 * half)
-                copy_g(b, 2 * half + 1)
-            if round_due(k - LAST_LAG) is not None:
-                store(round_due(k - LAST_LAG))
+            for b, j in g_tiles_due(k - 1):
+                if b > 0:
+                    copy_g(b, j)
+            if k == WEIGHT_TICK + 1:
+                copy_weights()
+            if round_due(k - Y_LAG - 2) is not None:
+                store(round_due(k - Y_LAG - 2))
 
-            if pair_due(k - PAIR) is not None:
-                reciprocal_sums(pair_due(k - PAIR))
-            if clip_due(k - AGG_LAG) is not None:
-                quantise_gT(clip_due(k - AGG_LAG))
-            if tile_due(k - NORM_LAG):
-                normalise(k - NORM_LAG)
+            for b, j in g_tiles_due(k - 2):
+                if b > 0:
+                    quantise_gT(b, j)
+            if k == WEIGHT_TICK + 2:
+                quantise_weights()
+            if round_due(k - Y_LAG - 1) is not None:
+                quantise_y(round_due(k - Y_LAG - 1))
+            if tile_due(k - GP_LAG):
+                quantise_gp(k - GP_LAG)
             if tile_due(k - QUANT_LAG):
                 quantise_e(k - QUANT_LAG)
-            if (k + MAX_LEAD) // ROUND + 1 < N_ROUNDS:
-                max_step((k + MAX_LEAD) // ROUND + 1, (k + MAX_LEAD) % ROUND)
-            if clip_half_due(k - 1) is not None:
-                regroup_g(*clip_half_due(k - 1))
-            if round_due(k - LAST_LAG + 2) is not None:
-                quantise_y(round_due(k - LAST_LAG + 2))
-            if clip_due(k - AGG_LAG - 1) is not None:
-                quantise_gp(clip_due(k - AGG_LAG - 1))
-
-            if tile_due(k - AGG_LAG):
-                aggregate(k - AGG_LAG)
-            if round_due(k - LAST_LAG + 1) is not None:
-                project(round_due(k - LAST_LAG + 1))
             if pair_due(k - PAIR) is not None:
-                spread_sums(pair_due(k - PAIR))
+                reciprocal_sums(pair_due(k - PAIR))
+            if pair_due(k - PAIR - 1) is not None:
+                copy_sums(pair_due(k - PAIR - 1))
+            if k == WEIGHT_TICK + 1:
+                add_biases()
+            if tile_due(k + MAX_LEAD):
+                maxima(k + MAX_LEAD)
+            first_g = [(b, j) for b, j in g_tiles_due(k - 1) if b == 0]
+            for b, j in first_g:
+                copy_g(b, j)
+            for b, j in first_g:
+                quantise_gT(b, j)
+            if tile_due(k - NORM_LAG):
+                normalise(k - NORM_LAG)
+
+            if tile_due(k - GP_LAG + 2):
+                regroup_g(k - GP_LAG + 2)
+
             if tile_due(k):
                 transpose_e(k)
-            if clip_half_due(k) is not None:
-                b, half = clip_half_due(k)
-                transpose_g(b, 2 * half)
-                transpose_g(b, 2 * half + 1)
+            for b, j in g_tiles_due(k):
+                transpose_g(b, j)
+            if k == WEIGHT_TICK:
+                transpose_weights()
+            if pair_due(k - PAIR) is not None:
+                spread_sums(pair_due(k - PAIR))
+            if round_due(k - Y_LAG - 1) is not None:
+                project(round_due(k - Y_LAG - 1))
+            if tile_due(k - AGG_LAG):
+                aggregate(k - AGG_LAG)

@@ -21,7 +21,8 @@ TILES = CLIPS * L_TILES
 M_PASSES = L // K_PASS
 F_TILES = FEAT // P
 ROUND = 4
-N_ROUNDS = TILES // ROUND
+GROUPS = [(k, ROUND) for k in range(0, TILES - ROUND, ROUND)] + [(TILES - 4, 2), (TILES - 2, 1), (TILES - 1, 1)]
+GROUP_OF = {k: (n, k - first) for n, (first, count) in enumerate(GROUPS) for k in range(first, first + count)}
 PAIR = 2
 N_PAIRS = TILES // PAIR
 
@@ -30,8 +31,8 @@ COPY_LAG = 1
 QUANT_LAG = 2
 AGG_LAG = 2
 NORM_LAG = 3
+FIRST_AGG = 3
 GP_LAG = 2
-Y_LAG = ROUND - 1 + NORM_LAG
 WEIGHT_TICK = 4
 
 FLOPS = 2 * CLIPS * (L * L * FEAT + 2 * L * FEAT * CH)
@@ -78,6 +79,8 @@ def tile_stnonlocalgnlstage_pb_t_kernel(tc, att_logits, g, w1_w, w1_b, w2_w, w2_
 
         warm = const.tile([P, 1], F32)
         nc.gpsimd.memset(warm[:], 0.0)
+        minus_one = const.tile([P, PAIR], F32)
+        nc.gpsimd.memset(minus_one[:], -1.0)
         nc.scalar.activation(out=warm[:], in_=warm[:], func=ACT.Exp)
 
         ident = const.tile([P, P], F32)
@@ -219,16 +222,20 @@ def tile_stnonlocalgnlstage_pb_t_kernel(tc, att_logits, g, w1_w, w1_b, w2_w, w2_
 
         def reciprocal_sums(h):
             e_rsum[h] = work.tile([P, PAIR], F32, name="e_rsum")
-            nc.vector.reciprocal(out=e_rsum[h][:], in_=e_sum[h][:])
+            nc.gpsimd.tensor_tensor(out=e_rsum[h][:], in0=e_sum[h][:], in1=minus_one[:], op=ALU.pow)
 
         def spread_sums(h):
             rsum_bank[h] = psum.tile([P, PAIR, P], F32, name="rsum_bank", bufs=1)
             for s in range(PAIR):
                 nc.tensor.transpose(rsum_bank[h][:, s, :], e_rsum[h][:, s : s + 1].to_broadcast([P, P]), ident[:])
 
+        def on_scalar(h):
+            return h % 4 < 1
+
         def copy_sums(h):
             rsum_all[h] = work.tile([P, PAIR, P], F32, name="rsum_all", bufs=3)
-            nc.vector.tensor_copy(out=rsum_all[h][:], in_=rsum_bank[h][:])
+            copy = nc.scalar.copy if on_scalar(h) else nc.vector.tensor_copy
+            copy(out=rsum_all[h][:], in_=rsum_bank[h][:])
 
         y_bank, y_grouped, y_codes, y_scales, out_bank = {}, {}, {}, {}, {}
 
@@ -248,28 +255,30 @@ def tile_stnonlocalgnlstage_pb_t_kernel(tc, att_logits, g, w1_w, w1_b, w2_w, w2_
                     )
 
         def normalise(k):
-            r, t = divmod(k, ROUND)
+            n, t = GROUP_OF[k]
             h, s = divmod(k, PAIR)
             if t == 0:
-                y_grouped[r] = work.tile([P, ROUND, P, PACK], BF16, name="y_grouped", align_bytes=64)
+                y_grouped[n] = work.tile([P, GROUPS[n][1], P, PACK], BF16, name="y_grouped", align_bytes=64)
             nc.vector.tensor_tensor(
-                out=y_grouped[r][:, t, :, :],
+                out=y_grouped[n][:, t, :, :],
                 in0=y_bank[k][:].rearrange("q j l -> q l j"),
                 in1=rsum_all[h][:, s, :].unsqueeze(2).to_broadcast([P, P, PACK]),
                 op=ALU.mult,
             )
 
-        def quantise_y(r):
-            y_codes[r] = work.tile([P, ROUND * P], U32, name="y_codes", align_bytes=64)
-            y_scales[r] = work.tile([P, ROUND * P], U8, name="y_scales", align_bytes=64)
-            quantise(y_grouped[r][:].rearrange("q t l j -> q (t l j)"), y_codes[r][:], y_scales[r][:])
+        def quantise_y(n):
+            width = GROUPS[n][1] * P
+            y_codes[n] = work.tile([P, width], U32, name="y_codes", align_bytes=64)
+            y_scales[n] = work.tile([P, width], U8, name="y_scales", align_bytes=64)
+            quantise(y_grouped[n][:].rearrange("q t l j -> q (t l j)"), y_codes[n][:], y_scales[n][:])
 
-        def project(r):
-            b, first = divmod(r * ROUND, L_TILES)
-            cols = slice(first * P, (first + ROUND) * P)
-            out_bank[r] = psum.tile([P, ROUND * P], F32, name="out_bank", bufs=1)
+        def project(n):
+            first, count = GROUPS[n]
+            b, i = divmod(first, L_TILES)
+            cols = slice(i * P, (i + count) * P)
+            out_bank[n] = psum.tile([P, count * P], F32, name="out_bank", bufs=1)
             nc.tensor.matmul_mx(
-                out=out_bank[r][:],
+                out=out_bank[n][:],
                 lhsT=w_codes[:, 0, :].bitcast(FP8X4),
                 lhsT_scale=w_scales[:, 0, :],
                 rhs=gp_codes[b][:, cols].bitcast(FP8X4),
@@ -278,27 +287,33 @@ def tile_stnonlocalgnlstage_pb_t_kernel(tc, att_logits, g, w1_w, w1_b, w2_w, w2_
                 stop=False,
             )
             nc.tensor.matmul_mx(
-                out=out_bank[r][:],
+                out=out_bank[n][:],
                 lhsT=w_codes[:, 1, :].bitcast(FP8X4),
                 lhsT_scale=w_scales[:, 1, :],
-                rhs=y_codes[r][:].bitcast(FP8X4),
-                rhs_scale=y_scales[r][:],
+                rhs=y_codes[n][:].bitcast(FP8X4),
+                rhs_scale=y_scales[n][:],
                 start=False,
                 stop=True,
             )
 
-        def store(r):
-            b, first = divmod(r * ROUND, L_TILES)
-            out_sb = work.tile([P, ROUND * P], F32)
-            nc.scalar.activation(out=out_sb[:], in_=out_bank[r][:], func=ACT.Identity, bias=bias[:, 0:1], scale=1.0)
-            nc.sync.dma_start(out=out[b, :, first * P : (first + ROUND) * P], in_=out_sb[:])
+        def store(n):
+            first, count = GROUPS[n]
+            b, i = divmod(first, L_TILES)
+            out_sb = work.tile([P, count * P], F32, name="out_sb", bufs=3)
+            nc.scalar.activation(out=out_sb[:], in_=out_bank[n][:], func=ACT.Identity, bias=bias[:, 0:1], scale=1.0)
+            nc.sync.dma_start(out=out[b, :, i * P : (i + count) * P], in_=out_sb[:])
 
         def tile_due(k):
             return 0 <= k < TILES
 
-        def round_due(tick):
-            r, t = divmod(tick, ROUND)
-            return r if t == 0 and 0 <= r < N_ROUNDS else None
+        def tiles_due(tick, lag, first):
+            if tick < first:
+                return []
+            return [k for k in (range(first - lag + 1) if tick == first else [tick - lag]) if tile_due(k)]
+
+        def group_due(k):
+            ends = [first + count - 1 for first, count in GROUPS]
+            return ends.index(k) if k in ends else None
 
         def pair_due(tick):
             h, s = divmod(tick, PAIR)
@@ -314,33 +329,33 @@ def tile_stnonlocalgnlstage_pb_t_kernel(tc, att_logits, g, w1_w, w1_b, w2_w, w2_
             b, j = divmod(tick + F_TILES, L_TILES)
             return [(b, j)] if 1 <= b < CLIPS and j < F_TILES else []
 
-        for k in range(-MAX_LEAD, TILES - ROUND + Y_LAG + 3):
+        for k in range(-MAX_LEAD, TILES + NORM_LAG + 2):
             if tile_due(k):
                 exponential(k)
             if tile_due(k - COPY_LAG):
                 copy_e(k - COPY_LAG)
+            if pair_due(k - PAIR - 1) is not None and on_scalar(pair_due(k - PAIR - 1)):
+                copy_sums(pair_due(k - PAIR - 1))
             for b, j in g_tiles_due(k - 1):
                 if b > 0:
                     copy_g(b, j)
             if k == WEIGHT_TICK + 1:
                 copy_weights()
-            if round_due(k - Y_LAG - 2) is not None:
-                store(round_due(k - Y_LAG - 2))
+            if group_due(k - NORM_LAG - 2) is not None:
+                store(group_due(k - NORM_LAG - 2))
 
             for b, j in g_tiles_due(k - 2):
                 if b > 0:
                     quantise_gT(b, j)
             if k == WEIGHT_TICK + 2:
                 quantise_weights()
-            if round_due(k - Y_LAG - 1) is not None:
-                quantise_y(round_due(k - Y_LAG - 1))
             if tile_due(k - GP_LAG):
                 quantise_gp(k - GP_LAG)
+            if group_due(k - NORM_LAG - 1) is not None:
+                quantise_y(group_due(k - NORM_LAG - 1))
             if tile_due(k - QUANT_LAG):
                 quantise_e(k - QUANT_LAG)
-            if pair_due(k - PAIR) is not None:
-                reciprocal_sums(pair_due(k - PAIR))
-            if pair_due(k - PAIR - 1) is not None:
+            if pair_due(k - PAIR - 1) is not None and not on_scalar(pair_due(k - PAIR - 1)):
                 copy_sums(pair_due(k - PAIR - 1))
             if k == WEIGHT_TICK + 1:
                 add_biases()
@@ -351,9 +366,11 @@ def tile_stnonlocalgnlstage_pb_t_kernel(tc, att_logits, g, w1_w, w1_b, w2_w, w2_
                 copy_g(b, j)
             for b, j in first_g:
                 quantise_gT(b, j)
-            if tile_due(k - NORM_LAG):
-                normalise(k - NORM_LAG)
+            for y in tiles_due(k, NORM_LAG, FIRST_AGG + 1):
+                normalise(y)
 
+            if pair_due(k - PAIR) is not None:
+                reciprocal_sums(pair_due(k - PAIR))
             if tile_due(k - GP_LAG + 2):
                 regroup_g(k - GP_LAG + 2)
 
@@ -365,7 +382,7 @@ def tile_stnonlocalgnlstage_pb_t_kernel(tc, att_logits, g, w1_w, w1_b, w2_w, w2_
                 transpose_weights()
             if pair_due(k - PAIR) is not None:
                 spread_sums(pair_due(k - PAIR))
-            if round_due(k - Y_LAG - 1) is not None:
-                project(round_due(k - Y_LAG - 1))
-            if tile_due(k - AGG_LAG):
-                aggregate(k - AGG_LAG)
+            if group_due(k - NORM_LAG - 1) is not None:
+                project(group_due(k - NORM_LAG - 1))
+            for y in tiles_due(k, AGG_LAG, FIRST_AGG):
+                aggregate(y)

@@ -31,6 +31,7 @@ COPY_LAG = 1
 QUANT_LAG = 2
 AGG_LAG = 2
 NORM_LAG = 3
+WARM = 1
 FIRST_AGG = 3
 GP_LAG = 2
 WEIGHT_TICK = 4
@@ -158,9 +159,16 @@ def tile_stnonlocalgnlstage_pb_t_kernel(tc, att_logits, g, w1_w, w1_b, w2_w, w2_
                 accum_out=e_sum[h][:, s : s + 1],
             )
 
+        def warm_up(bank, count):
+            for n in range(count):
+                nc.tensor.matmul(bank[:, n % 4, :], lhsT=ident[:], rhs=ident[:], start=True, stop=True)
+
         def transpose_e(k):
             e_words = e_sb[k][:].bitcast(F32)
-            e_bank[k] = transpose_pairs([e_words[:, n * P : (n + 1) * P] for n in range(4)], "e_bank")
+            e_bank[k] = psum.tile([P, 4, P], F32, name="e_bank")
+            warm_up(e_bank[k], WARM if k >= FIRST_AGG else 2 * WARM)
+            for n in range(4):
+                nc.tensor.transpose(e_bank[k][:, n, :], e_words[:, n * P : (n + 1) * P], ident[:])
 
         def copy_e(k):
             eT_grouped[k] = work.tile([P, M_PASSES * P * PACK], BF16, name="eT_grouped", align_bytes=64, bufs=3)

@@ -238,7 +238,7 @@ def tile_stnonlocalgnlstage_pb_t_kernel(tc, att_logits, g, w1_w, w1_b, w2_w, w2_
                 nc.tensor.transpose(rsum_bank[h][:, s, :], e_rsum[h][:, s : s + 1].to_broadcast([P, P]), ident[:])
 
         def on_scalar(h):
-            return h % 4 < 1
+            return h % 4 == 0 or h == N_PAIRS - 1
 
         def copy_sums(h):
             rsum_all[h] = work.tile([P, PAIR, P], F32, name="rsum_all", bufs=3)
@@ -284,7 +284,8 @@ def tile_stnonlocalgnlstage_pb_t_kernel(tc, att_logits, g, w1_w, w1_b, w2_w, w2_
             first, count = GROUPS[n]
             b, i = divmod(first, L_TILES)
             cols = slice(i * P, (i + count) * P)
-            out_bank[n] = psum.tile([P, count * P], F32, name="out_bank", bufs=1)
+            last = n == len(GROUPS) - 1
+            out_bank[n] = psum.tile([P, count * P], F32, name="out_bank", tag="g_bank" if last else "out_bank", bufs=2 if last else 1)
             nc.tensor.matmul_mx(
                 out=out_bank[n][:],
                 lhsT=w_codes[:, 0, :].bitcast(FP8X4),
@@ -314,14 +315,15 @@ def tile_stnonlocalgnlstage_pb_t_kernel(tc, att_logits, g, w1_w, w1_b, w2_w, w2_
         def tile_due(k):
             return 0 <= k < TILES
 
-        def tiles_due(tick, lag, first):
-            if tick < first:
-                return []
-            return [k for k in (range(first - lag + 1) if tick == first else [tick - lag]) if tile_due(k)]
+        def stage_tick(k, lag, first=0):
+            return max(k + lag - (k == TILES - 1), first)
 
-        def group_due(k):
-            ends = [first + count - 1 for first, count in GROUPS]
-            return ends.index(k) if k in ends else None
+        def tiles_due(tick, lag, first=0):
+            return [k for k in range(TILES) if stage_tick(k, lag, first) == tick]
+
+        def groups_due(tick, lag):
+            ends = [stage_tick(first + count - 1, NORM_LAG) for first, count in GROUPS]
+            return [n for n, end in enumerate(ends) if end + lag == tick]
 
         def pair_due(tick):
             h, s = divmod(tick, PAIR)
@@ -349,8 +351,8 @@ def tile_stnonlocalgnlstage_pb_t_kernel(tc, att_logits, g, w1_w, w1_b, w2_w, w2_
                     copy_g(b, j)
             if k == WEIGHT_TICK + 1:
                 copy_weights()
-            if group_due(k - NORM_LAG - 2) is not None:
-                store(group_due(k - NORM_LAG - 2))
+            for n in groups_due(k, 2):
+                store(n)
 
             for b, j in g_tiles_due(k - 2):
                 if b > 0:
@@ -359,10 +361,10 @@ def tile_stnonlocalgnlstage_pb_t_kernel(tc, att_logits, g, w1_w, w1_b, w2_w, w2_
                 quantise_weights()
             if tile_due(k - GP_LAG):
                 quantise_gp(k - GP_LAG)
-            if group_due(k - NORM_LAG - 1) is not None:
-                quantise_y(group_due(k - NORM_LAG - 1))
-            if tile_due(k - QUANT_LAG):
-                quantise_e(k - QUANT_LAG)
+            for n in groups_due(k, 1):
+                quantise_y(n)
+            for e in tiles_due(k, QUANT_LAG):
+                quantise_e(e)
             if pair_due(k - PAIR - 1) is not None and not on_scalar(pair_due(k - PAIR - 1)):
                 copy_sums(pair_due(k - PAIR - 1))
             if k == WEIGHT_TICK + 1:
@@ -390,7 +392,7 @@ def tile_stnonlocalgnlstage_pb_t_kernel(tc, att_logits, g, w1_w, w1_b, w2_w, w2_
                 transpose_weights()
             if pair_due(k - PAIR) is not None:
                 spread_sums(pair_due(k - PAIR))
-            if group_due(k - NORM_LAG - 1) is not None:
-                project(group_due(k - NORM_LAG - 1))
+            for n in groups_due(k, 1):
+                project(n)
             for y in tiles_due(k, AGG_LAG, FIRST_AGG):
                 aggregate(y)

from contextlib import ExitStack

import concourse.mybir as mybir
from concourse.masks import make_identity

F32 = mybir.dt.float32
BF16 = mybir.dt.bfloat16
U32 = mybir.dt.uint32
U8 = mybir.dt.uint8
FP8X4 = mybir.dt.float8_e4m3fn_x4
ALU = mybir.AluOpType
ACT = mybir.ActivationFunctionType
AXIS = mybir.AxisListType

P = 128
PACK = 4
K_PASS = P * PACK
CLIPS, L, FEAT, CH = 4, 1024, 512, 128
L_TILES = L // P
TILES = CLIPS * L_TILES
M_PASSES = L // K_PASS
F_TILES = FEAT // P
ROUND = 4
GROUPS = [(k, ROUND) for k in range(0, TILES - ROUND, ROUND)] + [(TILES - 4, 2), (TILES - 2, 1), (TILES - 1, 1)]
GROUP_OF = {k: (n, k - first) for n, (first, count) in enumerate(GROUPS) for k in range(first, first + count)}
PAIR = 2
N_PAIRS = TILES // PAIR

MAX_LEAD = 2
COPY_LAG = 1
QUANT_LAG = 2
AGG_LAG = 2
NORM_LAG = 3
WARM = 1
FIRST_AGG = 3
GP_LAG = 2
WEIGHT_TICK = 4

FLOPS = 2 * CLIPS * (L * L * FEAT + 2 * L * FEAT * CH)


def tile_stnonlocalgnlstage_pb_t_kernel(tc, att_logits, g, w1_w, w1_b, w2_w, w2_b, out):
    nc = tc.nc
    with ExitStack() as stack:
        const = stack.enter_context(tc.tile_pool(name="const", bufs=1))
        inputs = stack.enter_context(tc.tile_pool(name="inputs", bufs=1))
        work = stack.enter_context(tc.tile_pool(name="work", bufs=2))
        psum = stack.enter_context(tc.psum_pool(name="psum", bufs=2))
        stack.enter_context(tc.manual_schedule())

        a_sb = [inputs.tile([P, L_TILES, L], BF16, name="a%d" % b) for b in range(CLIPS)]
        g_sb = [inputs.tile([P, PACK, L], BF16, name="g%d" % b) for b in range(CLIPS)]
        w_sb = const.tile([P, 2, FEAT], BF16)
        bias_rows = const.tile([P, P], BF16)

        def load_logits(b, first, count):
            rows = att_logits[b].rearrange("(i p) m -> p i m", p=P)
            nc.sync.dma_start(out=a_sb[b][:, first : first + count, :], in_=rows[:, first : first + count, :])

        def load_values(b, first=0, count=PACK):
            rows = g[b].rearrange("(q j) m -> q j m", j=PACK)
            nc.sync.dma_start(out=g_sb[b][:, first : first + count, :], in_=rows[:, first : first + count, :])

        nc.gpsimd.memset(bias_rows[:], 0.0)
        for i in range(3):
            load_logits(0, i, 1)
        load_values(0, 0, 2)
        load_logits(0, 3, 1)
        load_values(0, 2, 2)
        load_logits(0, 4, 2)
        load_logits(0, 6, 2)
        nc.sync.dma_start(out=w_sb[:, 0, :], in_=w1_w)
        nc.sync.dma_start(out=w_sb[:, 1, :], in_=w2_w)
        nc.sync.dma_start(out=bias_rows[0:1, :], in_=w1_b.rearrange("(o c) -> o c", o=1))
        nc.sync.dma_start(out=bias_rows[1:2, :], in_=w2_b.rearrange("(o c) -> o c", o=1))
        for b in range(1, CLIPS):
            load_values(b)
            for first in range(0, L_TILES, ROUND):
                load_logits(b, first, ROUND)

        warm = const.tile([P, 1], F32)
        nc.gpsimd.memset(warm[:], 0.0)
        minus_one = const.tile([P, PAIR], F32)
        nc.gpsimd.memset(minus_one[:], -1.0)
        nc.scalar.activation(out=warm[:], in_=warm[:], func=ACT.Exp)

        ident = const.tile([P, P], F32)
        make_identity(nc, ident[:])
        ident_bf = const.tile([P, P], BF16)
        make_identity(nc, ident_bf[:])

        def transpose_pairs(blocks, tag):
            bank = psum.tile([P, 4, P], F32, name=tag, tag=tag)
            for n, block in enumerate(blocks):
                nc.tensor.transpose(bank[:, n, :], block, ident[:])
            return bank

        def copy_pairs(bank, grouped, copy=nc.scalar.copy):
            copy(out=grouped, in_=bank[:].rearrange("q (c u) r -> q c r u", u=2))

        def quantise(grouped, codes, scales):
            nc.vector.quantize_mx(out=codes.bitcast(FP8X4), scales=scales, in_=grouped)

        w_grouped = const.tile([P, 2 * CH * PACK], BF16, align_bytes=64)
        w_codes = const.tile([P, 2, CH], U32, align_bytes=64)
        w_scales = const.tile([P, 2, CH], U8, align_bytes=64)
        w_words = w_sb[:].rearrange("c w p -> c (w p)").bitcast(F32).rearrange("c (w q u) -> c w u q", w=2, u=2)
        bias = const.tile([P, 1], F32)
        w_bank, bias_cols = {}, {}

        def transpose_weights():
            w_bank[0] = transpose_pairs([w_words[:, w, u, :] for w in range(2) for u in range(2)], "g_bank")
            bias_cols[0] = psum.tile([P, P], BF16, name="bias_cols", tag="g_bank")
            nc.tensor.transpose(bias_cols[0][:], bias_rows[:], ident_bf[:])

        def copy_weights():
            copy_pairs(w_bank[0], w_grouped[:].bitcast(F32).rearrange("q (w c u) -> q w c u", w=2, u=2))

        def add_biases():
            nc.vector.tensor_reduce(out=bias[:], in_=bias_cols[0][:, 0:2], axis=AXIS.X, op=ALU.add)

        def quantise_weights():
            quantise(
                w_grouped[:],
                w_codes[:].rearrange("q w c -> q (w c)"),
                w_scales[:].rearrange("q w c -> q (w c)"),
            )

        neg_max = {}

        def maxima(k):
            b, i = divmod(k, L_TILES)
            negated = work.tile([P, L], BF16, name="negated")
            neg_max[k] = work.tile([P, 1], F32, name="neg_max", bufs=MAX_LEAD + 2)
            nc.vector.tensor_scalar(
                out=negated[:],
                in0=a_sb[b][:, i, :],
                scalar1=-1.0,
                scalar2=None,
                op0=ALU.mult,
                op1=ALU.min,
                accum_out=neg_max[k][:],
            )

        e_sum, e_sb, e_bank, eT_grouped, eT_codes, eT_scales = {}, {}, {}, {}, {}, {}

        def exponential(k):
            b, i = divmod(k, L_TILES)
            h, s = divmod(k, PAIR)
            if s == 0:
                e_sum[h] = work.tile([P, PAIR], F32, name="e_sum", bufs=3)
            e_sb[k] = work.tile([P, L], BF16, name="e_sb", bufs=3)
            nc.scalar.activation(
                out=e_sb[k][:],
                in_=a_sb[b][:, i, :],
                func=ACT.Exp,
                bias=neg_max[k][:],
                scale=1.0,
                accum_out=e_sum[h][:, s : s + 1],
            )

        def warm_up(bank, count):
            for n in range(count):
                nc.tensor.matmul(bank[:, n % 4, :], lhsT=ident[:], rhs=ident[:], start=True, stop=True)

        def transpose_e(k):
            e_words = e_sb[k][:].bitcast(F32)
            e_bank[k] = psum.tile([P, 4, P], F32, name="e_bank")
            warm_up(e_bank[k], WARM if k >= FIRST_AGG else 2 * WARM)
            for n in range(4):
                nc.tensor.transpose(e_bank[k][:, n, :], e_words[:, n * P : (n + 1) * P], ident[:])

        def copy_e(k):
            eT_grouped[k] = work.tile([P, M_PASSES * P * PACK], BF16, name="eT_grouped", align_bytes=64, bufs=3)
            copy_pairs(e_bank[k], eT_grouped[k][:].bitcast(F32).rearrange("q (c l u) -> q c l u", c=M_PASSES, u=2))

        def quantise_e(k):
            eT_codes[k] = work.tile([P, M_PASSES, P], U32, name="eT_codes", align_bytes=64, bufs=4)
            eT_scales[k] = work.tile([P, M_PASSES, P], U8, name="eT_scales", align_bytes=64, bufs=4)
            quantise(
                eT_grouped[k][:],
                eT_codes[k][:].rearrange("q c l -> q (c l)"),
                eT_scales[k][:].rearrange("q c l -> q (c l)"),
            )

        g_bank, gT_grouped, gT_codes, gT_scales, gp_grouped, gp_codes, gp_scales = {}, {}, {}, {}, {}, {}, {}

        def transpose_g(b, j):
            g_words = g_sb[b][:, j, :].bitcast(F32)
            g_bank[j] = transpose_pairs([g_words[:, n * P : (n + 1) * P] for n in range(4)], "g_bank")

        def copy_g(b, j):
            if j == 0:
                gT_grouped[b] = work.tile([P, M_PASSES * FEAT * PACK], BF16, name="gT_grouped", align_bytes=64, bufs=1)
            gT_words = gT_grouped[b][:].bitcast(F32).rearrange("q (j c f u) -> q j c f u", c=M_PASSES, j=F_TILES, u=2)
            copy_pairs(g_bank[j], gT_words[:, j, :, :, :], nc.vector.tensor_copy if b == 0 else nc.scalar.copy)

        def quantise_gT(b, j):
            if j == 0:
                gT_codes[b] = work.tile([P, F_TILES, M_PASSES, P], U32, name="gT_codes", align_bytes=64)
                gT_scales[b] = work.tile([P, F_TILES, M_PASSES, P], U8, name="gT_scales", align_bytes=64)
            width = M_PASSES * P * PACK
            quantise(
                gT_grouped[b][:, j * width : (j + 1) * width],
                gT_codes[b][:, j, :, :].rearrange("q c f -> q (c f)"),
                gT_scales[b][:, j, :, :].rearrange("q c f -> q (c f)"),
            )

        def regroup_g(k):
            b, i = divmod(k, L_TILES)
            gp_grouped[k] = work.tile([P, P, PACK], BF16, name="gp_grouped", align_bytes=64)
            nc.gpsimd.tensor_scalar(
                out=gp_grouped[k][:],
                in0=g_sb[b][:, :, i * P : (i + 1) * P].rearrange("q j l -> q l j"),
                scalar1=1.0,
                scalar2=0.0,
                op0=ALU.mult,
                op1=ALU.add,
            )

        def quantise_gp(k):
            b, i = divmod(k, L_TILES)
            if i == 0:
                gp_codes[b] = work.tile([P, L], U32, name="gp_codes", align_bytes=64)
                gp_scales[b] = work.tile([P, L], U8, name="gp_scales", align_bytes=64)
            cols = slice(i * P, (i + 1) * P)
            quantise(gp_grouped[k][:].rearrange("q l j -> q (l j)"), gp_codes[b][:, cols], gp_scales[b][:, cols])

        e_rsum, rsum_bank, rsum_all = {}, {}, {}

        def reciprocal_sums(h):
            e_rsum[h] = work.tile([P, PAIR], F32, name="e_rsum")
            nc.gpsimd.tensor_tensor(out=e_rsum[h][:], in0=e_sum[h][:], in1=minus_one[:], op=ALU.pow)

        def spread_sums(h):
            rsum_bank[h] = psum.tile([P, PAIR, P], F32, name="rsum_bank", bufs=1)
            for s in range(PAIR):
                nc.tensor.transpose(rsum_bank[h][:, s, :], e_rsum[h][:, s : s + 1].to_broadcast([P, P]), ident[:])

        def on_scalar(h):
            return h % 4 == 0 or h == N_PAIRS - 1

        def copy_sums(h):
            rsum_all[h] = work.tile([P, PAIR, P], F32, name="rsum_all", bufs=3)
            copy = nc.scalar.copy if on_scalar(h) else nc.vector.tensor_copy
            copy(out=rsum_all[h][:], in_=rsum_bank[h][:])

        y_bank, y_grouped, y_codes, y_scales, out_bank = {}, {}, {}, {}, {}

        def aggregate(k):
            b = k // L_TILES
            y_bank[k] = psum.tile([P, F_TILES, P], F32, name="y_bank")
            for j in range(F_TILES):
                for c in range(M_PASSES):
                    nc.tensor.matmul_mx(
                        out=y_bank[k][:, j, :],
                        lhsT=gT_codes[b][:, j, c, :].bitcast(FP8X4),
                        lhsT_scale=gT_scales[b][:, j, c, :],
                        rhs=eT_codes[k][:, c, :].bitcast(FP8X4),
                        rhs_scale=eT_scales[k][:, c, :],
                        start=(c == 0),
                        stop=(c == M_PASSES - 1),
                    )

        def normalise(k):
            n, t = GROUP_OF[k]
            h, s = divmod(k, PAIR)
            if t == 0:
                y_grouped[n] = work.tile([P, GROUPS[n][1], P, PACK], BF16, name="y_grouped", align_bytes=64)
            nc.vector.tensor_tensor(
                out=y_grouped[n][:, t, :, :],
                in0=y_bank[k][:].rearrange("q j l -> q l j"),
                in1=rsum_all[h][:, s, :].unsqueeze(2).to_broadcast([P, P, PACK]),
                op=ALU.mult,
            )

        def quantise_y(n):
            width = GROUPS[n][1] * P
            y_codes[n] = work.tile([P, width], U32, name="y_codes", align_bytes=64)
            y_scales[n] = work.tile([P, width], U8, name="y_scales", align_bytes=64)
            quantise(y_grouped[n][:].rearrange("q t l j -> q (t l j)"), y_codes[n][:], y_scales[n][:])

        def project(n):
            first, count = GROUPS[n]
            b, i = divmod(first, L_TILES)
            cols = slice(i * P, (i + count) * P)
            last = n == len(GROUPS) - 1
            out_bank[n] = psum.tile([P, count * P], F32, name="out_bank", tag="g_bank" if last else "out_bank", bufs=2 if last else 1)
            nc.tensor.matmul_mx(
                out=out_bank[n][:],
                lhsT=w_codes[:, 0, :].bitcast(FP8X4),
                lhsT_scale=w_scales[:, 0, :],
                rhs=gp_codes[b][:, cols].bitcast(FP8X4),
                rhs_scale=gp_scales[b][:, cols],
                start=True,
                stop=False,
            )
            nc.tensor.matmul_mx(
                out=out_bank[n][:],
                lhsT=w_codes[:, 1, :].bitcast(FP8X4),
                lhsT_scale=w_scales[:, 1, :],
                rhs=y_codes[n][:].bitcast(FP8X4),
                rhs_scale=y_scales[n][:],
                start=False,
                stop=True,
            )

        def store(n):
            first, count = GROUPS[n]
            b, i = divmod(first, L_TILES)
            out_sb = work.tile([P, count * P], F32, name="out_sb", bufs=3)
            nc.scalar.activation(out=out_sb[:], in_=out_bank[n][:], func=ACT.Identity, bias=bias[:, 0:1], scale=1.0)
            nc.sync.dma_start(out=out[b, :, i * P : (i + count) * P], in_=out_sb[:])

        def tile_due(k):
            return 0 <= k < TILES

        def stage_tick(k, lag, first=0):
            return max(k + lag - (k == TILES - 1), first)

        def tiles_due(tick, lag, first=0):
            return [k for k in range(TILES) if stage_tick(k, lag, first) == tick]

        def groups_due(tick, lag):
            ends = [stage_tick(first + count - 1, NORM_LAG) for first, count in GROUPS]
            return [n for n, end in enumerate(ends) if end + lag == tick]

        def pair_due(tick):
            h, s = divmod(tick, PAIR)
            return h if s == 0 and 0 <= h < N_PAIRS else None

        def clip_due(tick):
            b, i = divmod(tick, L_TILES)
            return b if i == 0 and 0 <= b < CLIPS else None

        def g_tiles_due(tick):
            if 0 <= tick < F_TILES // 2:
                return [(0, 2 * tick), (0, 2 * tick + 1)]
            b, j = divmod(tick + F_TILES, L_TILES)
            return [(b, j)] if 1 <= b < CLIPS and j < F_TILES else []

        for k in range(-MAX_LEAD, TILES + NORM_LAG + 2):
            if tile_due(k):
                exponential(k)
            if tile_due(k - COPY_LAG):
                copy_e(k - COPY_LAG)
            if pair_due(k - PAIR - 1) is not None and on_scalar(pair_due(k - PAIR - 1)):
                copy_sums(pair_due(k - PAIR - 1))
            for b, j in g_tiles_due(k - 1):
                if b > 0:
                    copy_g(b, j)
            if k == WEIGHT_TICK + 1:
                copy_weights()
            for n in groups_due(k, 2):
                store(n)

            for b, j in g_tiles_due(k - 2):
                if b > 0:
                    quantise_gT(b, j)
            if k == WEIGHT_TICK + 2:
                quantise_weights()
            if tile_due(k - GP_LAG):
                quantise_gp(k - GP_LAG)
            for n in groups_due(k, 1):
                quantise_y(n)
            for e in tiles_due(k, QUANT_LAG):
                quantise_e(e)
            if pair_due(k - PAIR - 1) is not None and not on_scalar(pair_due(k - PAIR - 1)):
                copy_sums(pair_due(k - PAIR - 1))
            if k == WEIGHT_TICK + 1:
                add_biases()
            if tile_due(k + MAX_LEAD):
                maxima(k + MAX_LEAD)
            first_g = [(b, j) for b, j in g_tiles_due(k - 1) if b == 0]
            for b, j in first_g:
                copy_g(b, j)
            for b, j in first_g:
                quantise_gT(b, j)
            for y in tiles_due(k, NORM_LAG, FIRST_AGG + 1):
                normalise(y)

            if pair_due(k - PAIR) is not None:
                reciprocal_sums(pair_due(k - PAIR))
            if tile_due(k - GP_LAG + 2):
                regroup_g(k - GP_LAG + 2)

            if tile_due(k):
                transpose_e(k)
            for b, j in g_tiles_due(k):
                transpose_g(b, j)
            if k == WEIGHT_TICK:
                transpose_weights()
            if pair_due(k - PAIR) is not None:
                spread_sums(pair_due(k - PAIR))
            for n in groups_due(k, 1):
                project(n)
            for y in tiles_due(k, AGG_LAG, FIRST_AGG):
                aggregate(y)
